import numpy as np
import ml_dtypes


def mxq(x, axis, fmt="e4m3"):
    dtype, down = {"e4m3": (ml_dtypes.float8_e4m3fn, 7), "e5m2": (ml_dtypes.float8_e5m2, 14)}[fmt]
    v = np.moveaxis(np.asarray(x, np.float32).astype(ml_dtypes.bfloat16).astype(np.float64), axis, -1)
    blocks = v.reshape(v.shape[:-1] + (-1, 32))
    amax = np.abs(blocks).max(-1, keepdims=True)
    byte = np.maximum(np.where(amax > 0, np.frexp(amax)[1] - 1 + 127, 0) - down, 1)
    scale = np.exp2(byte - 127.0)
    codes = (blocks / scale).astype(np.float32).astype(dtype).astype(np.float64)
    return np.moveaxis((codes * scale).reshape(v.shape), -1, axis)


WIDE = False


def mx_kscale(k):
    if not WIDE:
        return np.ones(k)
    levels = np.array([10, -10, 5, -5, 0])
    a = np.random.permutation(np.resize(levels, k // 512 * 4)).reshape(k // 512, 4)
    idx = np.arange(k)
    return np.exp2(a[idx // 512, idx % 128 // 32])


BF16 = ml_dtypes.bfloat16


def bf(x):
    return np.asarray(x, np.float32).astype(BF16)


def f64(x):
    return np.asarray(x).astype(np.float64)


E2M1 = np.array([0.0, 0.5, 1.0, 1.5, 2.0, 3.0, 4.0, 6.0, -0.0, -0.5, -1.0, -1.5, -2.0, -3.0, -4.0, -6.0])


def pack_weight(w, fmt):
    k, n = w.shape
    w = f64(bf(w)).reshape(k // 32, 32, n)
    amax = np.abs(w).max(1)
    if fmt == "e4m3":
        byte = np.frexp(amax)[1] - 1 + 127 - 7
    else:
        mant, ex = np.frexp(amax / 6.0)
        byte = np.where(mant > 0.5, ex, ex - 1) + 127
    byte = np.clip(np.where(amax > 0, byte, 1), 1, 254)
    scaled = (w * np.exp2(127.0 - byte)[:, None, :]).reshape(k, n).astype(np.float32)
    by_word = np.ascontiguousarray(scaled.reshape(k // 512, 128, 4, n).transpose(0, 1, 3, 2))
    if fmt == "e4m3":
        words = by_word.astype(ml_dtypes.float8_e4m3fn).view(np.uint8)
    else:
        c = by_word.astype(ml_dtypes.float4_e2m1fn).view(np.uint8) & 0xF
        words = c[..., 0::2] | (c[..., 1::2] << 4)
    return np.ascontiguousarray(words), np.ascontiguousarray(byte.astype(np.uint8).reshape(k // 512, 16, n))


def unpack_weight(words, scales, fmt):
    g, p, n, _ = words.shape
    if fmt == "e4m3":
        vals = np.ascontiguousarray(words).view(ml_dtypes.float8_e4m3fn).astype(np.float64)
    else:
        nib = np.empty((g, p, n, 4), np.uint8)
        nib[..., 0::2] = words & 0xF
        nib[..., 1::2] = words >> 4
        vals = E2M1[nib]
    vals = vals * np.repeat(np.exp2(scales.astype(np.float64) - 127.0), 8, axis=1)[..., None]
    return vals.transpose(0, 1, 3, 2).reshape(g * 512, n)


N, F, U, G, P = 1024, 512, 512, 3, 3
C = G + P
T = G + 2 * P + 1
LO, HI = -1.0, 1.0
LN_EPS = 0.001
FMT = "e4m3"


def b_splines(x, grid):
    xe = x[..., None]
    bases = np.where((xe >= grid[..., :-1]) & (xe < grid[..., 1:]), 1.0, 0.0)
    for k in range(1, P + 1):
        left = (xe - grid[..., :-(k + 1)]) / (grid[..., k:-1] - grid[..., :-(k + 1)])
        right = (grid[..., k + 1:] - xe) / (grid[..., k + 1:] - grid[..., 1:-k])
        bases = left * bases[..., :-1] + right * bases[..., 1:]
    return bases.reshape(x.shape[0], -1)


def setup_inputs():
    t = mx_kscale(F)
    h = (HI - LO) / G
    knots = np.linspace(LO - P * h, LO + (G + P) * h, T)
    grid = knots[None, None, :] + (np.random.random_sample((1, F, T)) - 0.5) * 0.25 * h
    x = bf(np.random.standard_normal((N, F)) * 0.1 + np.random.standard_normal((N, 1)) * 0.1)
    ln_gamma = bf((1.0 + 0.1 * np.random.standard_normal(F)) * t)
    ln_beta = bf(0.1 * np.random.standard_normal(F) * t)
    base_weight_words, base_weight_scales = pack_weight(np.random.standard_normal((F, U)) / np.sqrt(F) / t[:, None], FMT)
    base_bias = bf(0.25 * np.random.standard_normal(U))
    spline_weight_words, spline_weight_scales = pack_weight(np.random.standard_normal((F * C, U)) / np.sqrt(F), FMT)
    return {
        "x": x,
        "ln_gamma": ln_gamma,
        "ln_beta": ln_beta,
        "base_weight_words": base_weight_words,
        "base_weight_scales": base_weight_scales,
        "base_bias": base_bias,
        "spline_weight_words": spline_weight_words,
        "spline_weight_scales": spline_weight_scales,
        "grid": bf(grid * t[None, :, None]),
    }


def reference(x, ln_gamma, ln_beta, base_weight_words, base_weight_scales, base_bias, spline_weight_words, spline_weight_scales, grid):
    x = f64(x)
    mean = x.mean(-1, keepdims=True)
    var = x.var(-1, keepdims=True)
    xn = (x - mean) / np.sqrt(var + LN_EPS) * f64(ln_gamma) + f64(ln_beta)
    base_out = (mxq(np.maximum(xn, 0.0), 1, "e4m3") @ unpack_weight(base_weight_words, base_weight_scales, FMT)) + f64(base_bias)
    spline_out = mxq(b_splines(xn, f64(grid)), 1, "e4m3") @ unpack_weight(spline_weight_words, spline_weight_scales, FMT)
    return base_out + spline_out

@@ -1,0 +1,334 @@
+from contextlib import ExitStack
+
+import concourse.mybir as mybir
+from concourse.masks import make_identity
+
+F32 = mybir.dt.float32
+BF16 = mybir.dt.bfloat16
+I32 = mybir.dt.int32
+U32 = mybir.dt.uint32
+U8 = mybir.dt.uint8
+FP8X4 = mybir.dt.float8_e4m3fn_x4
+ALU = mybir.AluOpType
+ACT = mybir.ActivationFunctionType
+
+P = 128
+ROWS, FEATURES, UNITS = 1024, 512, 512
+BASES = 6
+KNOTS = 10
+LN_EPS = 0.001
+K_PASS = 512
+PASSES = (FEATURES + FEATURES * BASES) // K_PASS
+F_TILES = FEATURES // P
+CHUNK = 512
+R_TILES = CHUNK // P
+CHUNKS = ROWS // CHUNK
+UNITS_OF_WORK = [(c, a) for c in range(CHUNKS) for a in range(F_TILES)]
+
+FLOPS = 2 * ROWS * (FEATURES + FEATURES * BASES) * UNITS
+
+
+def tile_kanlinear_pa_kernel(
+    tc,
+    x,
+    ln_gamma,
+    ln_beta,
+    base_weight_words,
+    base_weight_scales,
+    base_bias,
+    spline_weight_words,
+    spline_weight_scales,
+    grid,
+    out,
+):
+    nc = tc.nc
+    with ExitStack() as stack:
+        const = stack.enter_context(tc.tile_pool(name="const", bufs=1))
+        work = stack.enter_context(tc.tile_pool(name="work", bufs=2))
+        psum = stack.enter_context(tc.psum_pool(name="psum", bufs=2))
+        stack.enter_context(tc.manual_schedule())
+
+        x_bf = const.tile([P, ROWS // P, FEATURES], BF16)
+        x_rows = x.rearrange("(r p) f -> p r f", p=P)
+        for c in range(CHUNKS):
+            r_range = slice(c * R_TILES, (c + 1) * R_TILES)
+            nc.sync.dma_start(out=x_bf[:, r_range, :], in_=x_rows[:, r_range, :])
+
+        knots_bf = const.tile([P, F_TILES, KNOTS], BF16)
+        gamma_bf = const.tile([P, F_TILES], BF16)
+        beta_bf = const.tile([P, F_TILES], BF16)
+        bias_bf = const.tile([P, UNITS], BF16)
+        with nc.allow_non_contiguous_dma(reason="small per-feature tables, one feature to a partition"):
+            nc.scalar.dma_start(out=knots_bf[:], in_=grid[0].rearrange("(a p) i -> p a i", p=P))
+            nc.scalar.dma_start(out=gamma_bf[:], in_=ln_gamma.rearrange("(a p) -> p a", p=P))
+            nc.scalar.dma_start(out=beta_bf[:], in_=ln_beta.rearrange("(a p) -> p a", p=P))
+        nc.scalar.dma_start(out=bias_bf[:], in_=base_bias.partition_broadcast(P))
+
+        w_words = const.tile([P, PASSES, 4 * UNITS], U8, align_bytes=64)
+        w_planes = const.tile([P, PASSES, UNITS], U8, align_bytes=64)
+        nc.vector.memset(w_planes[:].bitcast(I32), 0)
+        nc.sync.dma_start(
+            out=w_words[:, 0, :].bitcast(I32),
+            in_=base_weight_words[0].rearrange("p n t -> p (n t)").bitcast(I32),
+        )
+        nc.sync.dma_start(
+            out=w_words[:, 1:PASSES, :].bitcast(I32),
+            in_=spline_weight_words.rearrange("g p n t -> p g (n t)").bitcast(I32),
+        )
+        for quadrant in range(4):
+            live = slice(32 * quadrant, 32 * quadrant + 4)
+            scale_rows = slice(4 * quadrant, 4 * quadrant + 4)
+            nc.sync.dma_start(
+                out=w_planes[live, 0, :].bitcast(I32),
+                in_=base_weight_scales[0, scale_rows, :].bitcast(I32),
+            )
+            nc.sync.dma_start(
+                out=w_planes[live, 1:PASSES, :].bitcast(I32),
+                in_=spline_weight_scales[:, scale_rows, :].rearrange("g r n -> r g n").bitcast(I32),
+            )
+
+        ident_f32 = const.tile([P, P], F32)
+        make_identity(nc, ident_f32[:])
+        ident_bf = const.tile([P, P], BF16)
+        make_identity(nc, ident_bf[:])
+
+        gamma = const.tile([P, F_TILES], F32)
+        nc.vector.tensor_copy(out=gamma[:], in_=gamma_bf[:])
+        beta = const.tile([P, F_TILES], F32)
+        nc.vector.tensor_copy(out=beta[:], in_=beta_bf[:])
+        knot = const.tile([P, F_TILES, KNOTS + 1], F32)
+        nc.vector.tensor_copy(out=knot[:, :, 0:KNOTS], in_=knots_bf[:])
+        nc.vector.scalar_tensor_tensor(
+            out=knot[:, :, 10:11], in0=knot[:, :, 9:10], scalar=2.0, in1=knot[:, :, 8:9],
+            op0=ALU.mult, op1=ALU.subtract,
+        )
+        neg_knot = const.tile([P, F_TILES, KNOTS], F32)
+        nc.vector.tensor_scalar_mul(out=neg_knot[:], in0=knot[:, :, 0:KNOTS], scalar1=-1.0)
+
+        sigma = const.tile([P, F_TILES, 8], F32)
+        c1 = const.tile([P, F_TILES, BASES], F32)
+        c2 = const.tile([P, F_TILES, BASES], F32)
+        c4 = const.tile([P, F_TILES, BASES], F32)
+
+        def spline_constants():
+            gap = {}
+            inv = {}
+            for span in (1, 2, 3, 4):
+                count = KNOTS + 1 - span
+                gap[span] = const.tile([P, F_TILES, count], F32, name="gap%d" % span)
+                nc.vector.tensor_sub(out=gap[span][:], in0=knot[:, :, span : KNOTS + 1], in1=knot[:, :, 0:count])
+                inv[span] = const.tile([P, F_TILES, count], F32, name="inv%d" % span)
+                nc.vector.reciprocal(out=inv[span][:], in_=gap[span][:])
+            nc.vector.tensor_mul(out=sigma[:], in0=inv[1][:, :, 0:8], in1=inv[2][:, :, 0:8])
+            nc.vector.tensor_mul(out=sigma[:], in0=sigma[:], in1=inv[3][:, :, 0:8])
+            nc.vector.scalar_tensor_tensor(
+                out=c1[:], in0=gap[4][:, :, 0:6], scalar=-1.0, in1=inv[1][:, :, 0:6], op0=ALU.mult, op1=ALU.mult
+            )
+            nc.vector.tensor_mul(out=c2[:], in0=gap[4][:, :, 0:6], in1=inv[2][:, :, 0:6])
+            nc.vector.tensor_mul(out=c2[:], in0=c2[:], in1=inv[1][:, :, 1:7])
+            nc.vector.tensor_mul(out=c2[:], in0=c2[:], in1=gap[3][:, :, 2:8])
+            nc.vector.scalar_tensor_tensor(
+                out=c4[:], in0=inv[3][:, :, 1:7], scalar=-1.0, in1=inv[2][:, :, 2:8], op0=ALU.mult, op1=ALU.mult
+            )
+            nc.vector.tensor_mul(out=c4[:], in0=c4[:], in1=inv[1][:, :, 3:9])
+
+
+        mean_var = {}
+        rstd = {}
+        z = {}
+        xn = {}
+        relu_xn = {}
+        square = {}
+        cube = {}
+        pos = {}
+        bases = {}
+        rows = {}
+        grouped = {}
+        codes = {}
+        planes = {}
+        acc = {}
+
+        def statistics(c):
+            stats = work.tile([P, R_TILES, 6], F32, name="stats")
+            mean_var[c] = work.tile([P, R_TILES, 2], F32, name="mean_var")
+            for r in range(R_TILES):
+                nc.vector.bn_stats(out=stats[:, r, :], in_=x_bf[:, c * R_TILES + r, :])
+                nc.vector.bn_aggr(out=mean_var[c][:, r, :], in_=stats[:, r, :])
+
+        def normalise(c):
+            var_eps = work.tile([P, R_TILES], F32, name="var_eps")
+            nc.vector.tensor_scalar_add(out=var_eps[:], in0=mean_var[c][:, :, 1], scalar1=LN_EPS)
+            std = work.tile([P, R_TILES], F32, name="std")
+            nc.scalar.activation(out=std[:], in_=var_eps[:], func=ACT.Sqrt)
+            rstd0 = work.tile([P, R_TILES], F32, name="rstd0")
+            nc.vector.reciprocal(out=rstd0[:], in_=std[:])
+            newton = work.tile([P, R_TILES], F32, name="newton")
+            nc.vector.tensor_mul(out=newton[:], in0=rstd0[:], in1=rstd0[:])
+            nc.vector.tensor_mul(out=newton[:], in0=newton[:], in1=var_eps[:])
+            nc.vector.tensor_scalar(
+                out=newton[:], in0=newton[:], scalar1=-0.5, scalar2=1.5, op0=ALU.mult, op1=ALU.add
+            )
+            rstd[c] = work.tile([P, R_TILES], F32, name="rstd")
+            nc.vector.tensor_mul(out=rstd[c][:], in0=rstd0[:], in1=newton[:])
+            for r in range(R_TILES):
+                z[c, r] = work.tile([P, FEATURES], F32, name="z", bufs=ROWS // P)
+                nc.vector.tensor_scalar(
+                    out=z[c, r][:], in0=x_bf[:, c * R_TILES + r, :],
+                    scalar1=mean_var[c][:, r, 0:1], scalar2=rstd[c][:, r : r + 1],
+                    op0=ALU.subtract, op1=ALU.mult,
+                )
+
+        def features_to_partitions(c, a):
+            if a == 0:
+                relu_xn[c] = work.tile([P, F_TILES, CHUNK], BF16, name="relu_xn")
+            z_t = psum.tile([P, CHUNK], F32, name="z_t", bufs=1)
+            for r in range(R_TILES):
+                nc.tensor.transpose(z_t[:, r * P : (r + 1) * P], z[c, r][:, a * P : (a + 1) * P], ident_f32[:])
+            xn[c, a] = work.tile([P, CHUNK], F32, name="xn", bufs=3)
+            nc.scalar.activation(
+                out=xn[c, a][:], in_=z_t[:], func=ACT.Identity, scale=gamma[:, a : a + 1], bias=beta[:, a : a + 1]
+            )
+            nc.scalar.activation(
+                out=relu_xn[c][:, a, :], in_=z_t[:], func=ACT.Relu, scale=gamma[:, a : a + 1], bias=beta[:, a : a + 1]
+            )
+
+        def squares(c, a):
+            for i in range(KNOTS):
+                square[i] = work.tile([P, CHUNK], F32, name="square%d" % i, bufs=1)
+                nc.scalar.activation(out=square[i][:], in_=xn[c, a][:], func=ACT.Square, bias=neg_knot[:, a, i : i + 1])
+
+        def cubes(c, a):
+            for i in range(KNOTS):
+                cube[i] = work.tile([P, CHUNK], F32, name="cube%d" % i, bufs=1)
+                nc.vector.scalar_tensor_tensor(
+                    out=cube[i][:], in0=xn[c, a][:], scalar=knot[:, a, i : i + 1], in1=square[i][:],
+                    op0=ALU.subtract, op1=ALU.mult,
+                )
+                if i < 8:
+                    pos[i] = work.tile([P, CHUNK], F32, name="pos%d" % i, bufs=1)
+                    nc.scalar.activation(out=pos[i][:], in_=cube[i][:], func=ACT.Relu, scale=sigma[:, a, i : i + 1])
+
+        def combine(c, a):
+            left = {}
+            for j in range(BASES):
+                left[j] = work.tile([P, CHUNK], F32, name="left%d" % j, bufs=1)
+                nc.vector.scalar_tensor_tensor(
+                    out=left[j][:], in0=pos[j + 2][:], scalar=c2[:, a, j : j + 1], in1=pos[j][:],
+                    op0=ALU.mult, op1=ALU.add,
+                )
+            for j in range(BASES):
+                nc.vector.scalar_tensor_tensor(
+                    out=left[j][:], in0=pos[j + 1][:], scalar=c1[:, a, j : j + 1], in1=left[j][:],
+                    op0=ALU.mult, op1=ALU.add,
+                )
+            bases[c, a] = work.tile([P, BASES, CHUNK], BF16, name="bases", bufs=2)
+            for j in range(BASES):
+                nc.vector.scalar_tensor_tensor(
+                    out=bases[c, a][:, j, :], in0=cube[j + 4][:], scalar=c4[:, a, j : j + 1], in1=left[j][:],
+                    op0=ALU.mult, op1=ALU.min,
+                )
+
+        def bases_to_rows(c, a):
+            first = FEATURES + a * P * BASES
+            for r in range(R_TILES):
+                if a == 0:
+                    rows[c, r] = work.tile([P, PASSES * K_PASS], BF16, name="rows", bufs=R_TILES)
+                back = psum.tile([P, BASES * P], BF16, name="back")
+                for j in range(BASES):
+                    nc.tensor.transpose(back[:, j * P : (j + 1) * P], bases[c, a][:, j, r * P : (r + 1) * P], ident_bf[:])
+                nc.scalar.activation(
+                    out=rows[c, r][:, first : first + P * BASES].rearrange("n (f j) -> n f j", j=BASES),
+                    in_=back[:].rearrange("n (j f) -> n f j", j=BASES),
+                    func=ACT.Relu,
+                )
+
+        def relu_to_rows(c):
+            for r in range(R_TILES):
+                back = psum.tile([P, BASES * P], BF16, name="back")
+                for a in range(F_TILES):
+                    nc.tensor.transpose(back[:, a * P : (a + 1) * P], relu_xn[c][:, a, r * P : (r + 1) * P], ident_bf[:])
+                nc.scalar.copy(out=rows[c, r][:, 0:FEATURES], in_=back[:, 0:FEATURES])
+
+        def k_to_partitions(c, g):
+            grouped[g] = work.tile([P, 4 * CHUNK], BF16, name="grouped", align_bytes=64, bufs=3)
+            grouped_words = grouped[g][:].bitcast(F32).rearrange("p (n u) -> p n u", u=2)
+            for pair in range(R_TILES // 2):
+                k_t = psum.tile([P, 2, 2, P], F32, name="k_t")
+                for rr in range(2):
+                    row_words = rows[c, 2 * pair + rr][:].bitcast(F32)
+                    for u in range(2):
+                        nc.tensor.transpose(
+                            k_t[:, rr, u, :], row_words[:, 256 * g + u : 256 * (g + 1) : 2], ident_f32[:]
+                        )
+                nc.scalar.copy(
+                    out=grouped_words[:, 2 * pair * P : 2 * (pair + 1) * P, :].rearrange("p (rr n) u -> p rr n u", rr=2),
+                    in_=k_t[:].rearrange("p rr u n -> p rr n u"),
+                )
+
+        def quantise(c, g):
+            nc.vector.quantize_mx(out=codes[c][:, g, :].bitcast(FP8X4), scales=planes[c][:, g, :], in_=grouped[g][:])
+
+        def multiply(c, r):
+            acc[r] = psum.tile([P, UNITS], F32, name="acc")
+            n_cols = slice(r * P, (r + 1) * P)
+            for g in range(PASSES):
+                nc.tensor.matmul_mx(
+                    out=acc[r][:],
+                    lhsT=codes[c][:, g, n_cols].bitcast(FP8X4),
+                    lhsT_scale=planes[c][:, g, n_cols],
+                    rhs=w_words[:, g, :].bitcast(FP8X4),
+                    rhs_scale=w_planes[:, g, :],
+                    start=(g == 0),
+                    stop=(g == PASSES - 1),
+                )
+
+        def add_bias_and_store(c, r):
+            result = work.tile([P, UNITS], F32, name="result")
+            nc.vector.tensor_add(out=result[:], in0=acc[r][:], in1=bias_bf[:])
+            row0 = (c * R_TILES + r) * P
+            nc.sync.dma_start(out=out[row0 : row0 + P, :], in_=result[:])
+
+        def passes_after(a):
+            first = 1 + (a * P * BASES) // K_PASS
+            last = ((a + 1) * P * BASES) // K_PASS
+            return list(range(first, last + 1)) + ([0] if a == 2 else [])
+
+        statistics(0)
+        normalise(0)
+        spline_constants()
+        features_to_partitions(0, 0)
+        squares(0, 0)
+        statistics(1)
+        n_units = len(UNITS_OF_WORK)
+        for t in range(n_units + 3):
+            if t < n_units:
+                cubes(*UNITS_OF_WORK[t])
+            ready = []
+            if 1 <= t <= n_units:
+                pc, pa = UNITS_OF_WORK[t - 1]
+                if pa == 0:
+                    codes[pc] = work.tile([P, PASSES, CHUNK], U32, name="codes", align_bytes=64)
+                    planes[pc] = work.tile([P, PASSES, CHUNK], U8, name="planes", align_bytes=64)
+                bases_to_rows(pc, pa)
+                if pa == 2:
+                    relu_to_rows(pc)
+                ready = passes_after(pa)
+                for g in ready:
+                    k_to_partitions(pc, g)
+            if t + 1 < n_units:
+                features_to_partitions(*UNITS_OF_WORK[t + 1])
+                squares(*UNITS_OF_WORK[t + 1])
+            if t < n_units:
+                combine(*UNITS_OF_WORK[t])
+            if t == 0:
+                normalise(1)
+            for g in ready:
+                quantise(pc, g)
+            if t >= F_TILES:
+                done, step = divmod(t - F_TILES, F_TILES)
+                if 1 <= step <= 2:
+                    add_bias_and_store(done, 2 * step - 2)
+                    add_bias_and_store(done, 2 * step - 1)
+                if step <= 1:
+                    multiply(done, 2 * step)
+                    multiply(done, 2 * step + 1)

@@ -50,9 +50,9 @@ def tile_kanlinear_pa_kernel(
 
         x_bf = const.tile([P, ROWS // P, FEATURES], BF16)
         x_rows = x.rearrange("(r p) f -> p r f", p=P)
-        for c in range(CHUNKS):
-            r_range = slice(c * R_TILES, (c + 1) * R_TILES)
-            nc.sync.dma_start(out=x_bf[:, r_range, :], in_=x_rows[:, r_range, :])
+        for r in range(R_TILES):
+            nc.sync.dma_start(out=x_bf[:, r, :], in_=x_rows[:, r, :])
+        nc.sync.dma_start(out=x_bf[:, R_TILES:, :], in_=x_rows[:, R_TILES:, :])
 
         knots_bf = const.tile([P, F_TILES, KNOTS], BF16)
         gamma_bf = const.tile([P, F_TILES], BF16)
@@ -93,17 +93,19 @@ def tile_kanlinear_pa_kernel(
         make_identity(nc, ident_bf[:])
 
         gamma = const.tile([P, F_TILES], F32)
-        nc.vector.tensor_copy(out=gamma[:], in_=gamma_bf[:])
         beta = const.tile([P, F_TILES], F32)
-        nc.vector.tensor_copy(out=beta[:], in_=beta_bf[:])
         knot = const.tile([P, F_TILES, KNOTS + 1], F32)
-        nc.vector.tensor_copy(out=knot[:, :, 0:KNOTS], in_=knots_bf[:])
-        nc.vector.scalar_tensor_tensor(
-            out=knot[:, :, 10:11], in0=knot[:, :, 9:10], scalar=2.0, in1=knot[:, :, 8:9],
-            op0=ALU.mult, op1=ALU.subtract,
-        )
         neg_knot = const.tile([P, F_TILES, KNOTS], F32)
-        nc.vector.tensor_scalar_mul(out=neg_knot[:], in0=knot[:, :, 0:KNOTS], scalar1=-1.0)
+
+        def norm_constants():
+            nc.vector.tensor_copy(out=gamma[:], in_=gamma_bf[:])
+            nc.vector.tensor_copy(out=beta[:], in_=beta_bf[:])
+            nc.vector.tensor_copy(out=knot[:, :, 0:KNOTS], in_=knots_bf[:])
+            nc.vector.scalar_tensor_tensor(
+                out=knot[:, :, 10:11], in0=knot[:, :, 9:10], scalar=2.0, in1=knot[:, :, 8:9],
+                op0=ALU.mult, op1=ALU.subtract,
+            )
+            nc.vector.tensor_scalar_mul(out=neg_knot[:], in0=knot[:, :, 0:KNOTS], scalar1=-1.0)
 
         sigma = const.tile([P, F_TILES, 8], F32)
         c1 = const.tile([P, F_TILES, BASES], F32)
@@ -181,7 +183,7 @@ def tile_kanlinear_pa_kernel(
         def features_to_partitions(c, a):
             if a == 0:
                 relu_xn[c] = work.tile([P, F_TILES, CHUNK], BF16, name="relu_xn")
-            z_t = psum.tile([P, CHUNK], F32, name="z_t", bufs=1)
+            z_t = psum.tile([P, CHUNK], F32, name="z_t", tag="turned")
             for r in range(R_TILES):
                 nc.tensor.transpose(z_t[:, r * P : (r + 1) * P], z[c, r][:, a * P : (a + 1) * P], ident_f32[:])
             xn[c, a] = work.tile([P, CHUNK], F32, name="xn", bufs=3)
@@ -228,7 +230,7 @@ def tile_kanlinear_pa_kernel(
                     op0=ALU.mult, op1=ALU.min,
                 )
 
-        def bases_to_rows(c, a):
+        def bases_to_rows(c, a, vector_helps):
             first = FEATURES + a * P * BASES
             for r in range(R_TILES):
                 if a == 0:
@@ -236,11 +238,15 @@ def tile_kanlinear_pa_kernel(
                 back = psum.tile([P, BASES * P], BF16, name="back")
                 for j in range(BASES):
                     nc.tensor.transpose(back[:, j * P : (j + 1) * P], bases[c, a][:, j, r * P : (r + 1) * P], ident_bf[:])
-                nc.scalar.activation(
-                    out=rows[c, r][:, first : first + P * BASES].rearrange("n (f j) -> n f j", j=BASES),
-                    in_=back[:].rearrange("n (j f) -> n f j", j=BASES),
-                    func=ACT.Relu,
-                )
+                by_feature = rows[c, r][:, first : first + P * BASES].rearrange("n (f j) -> n f j", j=BASES)
+                if vector_helps and r % 2 == 1:
+                    nc.vector.tensor_scalar_max(
+                        out=by_feature, in0=back[:].rearrange("n (j f) -> n f j", j=BASES), scalar1=0.0
+                    )
+                else:
+                    nc.scalar.activation(
+                        out=by_feature, in_=back[:].rearrange("n (j f) -> n f j", j=BASES), func=ACT.Relu
+                    )
 
         def relu_to_rows(c):
             for r in range(R_TILES):
@@ -249,72 +255,82 @@ def tile_kanlinear_pa_kernel(
                     nc.tensor.transpose(back[:, a * P : (a + 1) * P], relu_xn[c][:, a, r * P : (r + 1) * P], ident_bf[:])
                 nc.scalar.copy(out=rows[c, r][:, 0:FEATURES], in_=back[:, 0:FEATURES])
 
-        def k_to_partitions(c, g):
+        def k_to_partitions(c, g, vector_helps):
             grouped[g] = work.tile([P, 4 * CHUNK], BF16, name="grouped", align_bytes=64, bufs=3)
             grouped_words = grouped[g][:].bitcast(F32).rearrange("p (n u) -> p n u", u=2)
             for pair in range(R_TILES // 2):
-                k_t = psum.tile([P, 2, 2, P], F32, name="k_t")
+                k_t = psum.tile([P, 2, 2, P], F32, name="k_t", tag="turned")
                 for rr in range(2):
                     row_words = rows[c, 2 * pair + rr][:].bitcast(F32)
                     for u in range(2):
                         nc.tensor.transpose(
                             k_t[:, rr, u, :], row_words[:, 256 * g + u : 256 * (g + 1) : 2], ident_f32[:]
                         )
-                nc.scalar.copy(
-                    out=grouped_words[:, 2 * pair * P : 2 * (pair + 1) * P, :].rearrange("p (rr n) u -> p rr n u", rr=2),
-                    in_=k_t[:].rearrange("p rr u n -> p rr n u"),
+                side_by_side = grouped_words[:, 2 * pair * P : 2 * (pair + 1) * P, :].rearrange(
+                    "p (rr n) u -> p rr n u", rr=2
                 )
+                if vector_helps and pair % 2 == 1:
+                    nc.vector.tensor_copy(out=side_by_side, in_=k_t[:].rearrange("p rr u n -> p rr n u"))
+                else:
+                    nc.scalar.copy(out=side_by_side, in_=k_t[:].rearrange("p rr u n -> p rr n u"))
 
         def quantise(c, g):
             nc.vector.quantize_mx(out=codes[c][:, g, :].bitcast(FP8X4), scales=planes[c][:, g, :], in_=grouped[g][:])
-
-        def multiply(c, r):
-            acc[r] = psum.tile([P, UNITS], F32, name="acc")
-            n_cols = slice(r * P, (r + 1) * P)
-            for g in range(PASSES):
-                nc.tensor.matmul_mx(
-                    out=acc[r][:],
-                    lhsT=codes[c][:, g, n_cols].bitcast(FP8X4),
-                    lhsT_scale=planes[c][:, g, n_cols],
-                    rhs=w_words[:, g, :].bitcast(FP8X4),
-                    rhs_scale=w_planes[:, g, :],
-                    start=(g == 0),
-                    stop=(g == PASSES - 1),
-                )
-
-        def add_bias_and_store(c, r):
-            result = work.tile([P, UNITS], F32, name="result")
-            nc.vector.tensor_add(out=result[:], in0=acc[r][:], in1=bias_bf[:])
-            row0 = (c * R_TILES + r) * P
-            nc.sync.dma_start(out=out[row0 : row0 + P, :], in_=result[:])
 
         def passes_after(a):
             first = 1 + (a * P * BASES) // K_PASS
             last = ((a + 1) * P * BASES) // K_PASS
             return list(range(first, last + 1)) + ([0] if a == 2 else [])
 
+        first_pass = passes_after(0)[0]
+        last_pass = passes_after(F_TILES - 1)[-1]
+
+        def multiply(c, g):
+            for r in range(R_TILES):
+                if g == first_pass:
+                    acc[r] = psum.tile([P, UNITS], F32, name="acc", bufs=R_TILES)
+                n_cols = slice(r * P, (r + 1) * P)
+                nc.tensor.matmul_mx(
+                    out=acc[r][:],
+                    lhsT=codes[c][:, g, n_cols].bitcast(FP8X4),
+                    lhsT_scale=planes[c][:, g, n_cols],
+                    rhs=w_words[:, g, :].bitcast(FP8X4),
+                    rhs_scale=w_planes[:, g, :],
+                    start=(g == first_pass),
+                    stop=(g == last_pass),
+                )
+
+        def add_bias_and_store(c):
+            for r in range(R_TILES):
+                result = work.tile([P, UNITS], F32, name="result")
+                nc.vector.tensor_add(out=result[:], in0=acc[r][:], in1=bias_bf[:])
+                row0 = (c * R_TILES + r) * P
+                nc.sync.dma_start(out=out[row0 : row0 + P, :], in_=result[:])
+
         statistics(0)
+        norm_constants()
         normalise(0)
         spline_constants()
         features_to_partitions(0, 0)
         squares(0, 0)
         statistics(1)
         n_units = len(UNITS_OF_WORK)
-        for t in range(n_units + 3):
+        for t in range(n_units + 1):
+            last_step = t == n_units
             if t < n_units:
                 cubes(*UNITS_OF_WORK[t])
             ready = []
-            if 1 <= t <= n_units:
+            if t >= 1:
                 pc, pa = UNITS_OF_WORK[t - 1]
                 if pa == 0:
                     codes[pc] = work.tile([P, PASSES, CHUNK], U32, name="codes", align_bytes=64)
                     planes[pc] = work.tile([P, PASSES, CHUNK], U8, name="planes", align_bytes=64)
-                bases_to_rows(pc, pa)
+                bases_to_rows(pc, pa, last_step)
                 if pa == 2:
                     relu_to_rows(pc)
                 ready = passes_after(pa)
                 for g in ready:
-                    k_to_partitions(pc, g)
+                    k_to_partitions(pc, g, last_step)
             if t + 1 < n_units:
                 features_to_partitions(*UNITS_OF_WORK[t + 1])
                 squares(*UNITS_OF_WORK[t + 1])
@@ -322,13 +338,9 @@ def tile_kanlinear_pa_kernel(
                 combine(*UNITS_OF_WORK[t])
             if t == 0:
                 normalise(1)
+            if t >= 1 and pa == 0 and pc >= 1:
+                add_bias_and_store(pc - 1)
             for g in ready:
                 quantise(pc, g)
-            if t >= F_TILES:
-                done, step = divmod(t - F_TILES, F_TILES)
-                if 1 <= step <= 2:
-                    add_bias_and_store(done, 2 * step - 2)
-                    add_bias_and_store(done, 2 * step - 1)
-                if step <= 1:
-                    multiply(done, 2 * step)
-                    multiply(done, 2 * step + 1)
+                multiply(pc, g)
+        add_bias_and_store(CHUNKS - 1)

@@ -50,9 +50,9 @@ def tile_kanlinear_pa_kernel(
 
         x_bf = const.tile([P, ROWS // P, FEATURES], BF16)
         x_rows = x.rearrange("(r p) f -> p r f", p=P)
-        for r in range(R_TILES):
-            nc.sync.dma_start(out=x_bf[:, r, :], in_=x_rows[:, r, :])
-        nc.sync.dma_start(out=x_bf[:, R_TILES:, :], in_=x_rows[:, R_TILES:, :])
+        for c in range(CHUNKS):
+            r_range = slice(c * R_TILES, (c + 1) * R_TILES)
+            nc.sync.dma_start(out=x_bf[:, r_range, :], in_=x_rows[:, r_range, :])
 
         knots_bf = const.tile([P, F_TILES, KNOTS], BF16)
         gamma_bf = const.tile([P, F_TILES], BF16)
@@ -93,50 +93,48 @@ def tile_kanlinear_pa_kernel(
         make_identity(nc, ident_bf[:])
 
         gamma = const.tile([P, F_TILES], F32)
+        nc.gpsimd.tensor_copy(out=gamma[:], in_=gamma_bf[:])
         beta = const.tile([P, F_TILES], F32)
+        nc.gpsimd.tensor_copy(out=beta[:], in_=beta_bf[:])
         knot = const.tile([P, F_TILES, KNOTS + 1], F32)
+        nc.gpsimd.tensor_copy(out=knot[:, :, 0:KNOTS], in_=knots_bf[:])
+        nc.gpsimd.tensor_sub(out=knot[:, :, 10:11], in0=knot[:, :, 9:10], in1=knot[:, :, 8:9])
+        nc.gpsimd.tensor_add(out=knot[:, :, 10:11], in0=knot[:, :, 10:11], in1=knot[:, :, 9:10])
         neg_knot = const.tile([P, F_TILES, KNOTS], F32)
-
-        def norm_constants():
-            nc.vector.tensor_copy(out=gamma[:], in_=gamma_bf[:])
-            nc.vector.tensor_copy(out=beta[:], in_=beta_bf[:])
-            nc.vector.tensor_copy(out=knot[:, :, 0:KNOTS], in_=knots_bf[:])
-            nc.vector.scalar_tensor_tensor(
-                out=knot[:, :, 10:11], in0=knot[:, :, 9:10], scalar=2.0, in1=knot[:, :, 8:9],
-                op0=ALU.mult, op1=ALU.subtract,
-            )
-            nc.vector.tensor_scalar_mul(out=neg_knot[:], in0=knot[:, :, 0:KNOTS], scalar1=-1.0)
-
+        nc.gpsimd.tensor_scalar(
+            out=neg_knot[:], in0=knot[:, :, 0:KNOTS], scalar1=-1.0, scalar2=0.0, op0=ALU.mult, op1=ALU.add
+        )
+        gap = {}
+        inv = {}
+        for span in (1, 2, 3, 4):
+            count = KNOTS + 1 - span
+            gap[span] = const.tile([P, F_TILES, count], F32, name="gap%d" % span)
+            nc.gpsimd.tensor_sub(out=gap[span][:], in0=knot[:, :, span : KNOTS + 1], in1=knot[:, :, 0:count])
         sigma = const.tile([P, F_TILES, 8], F32)
         c1 = const.tile([P, F_TILES, BASES], F32)
         c2 = const.tile([P, F_TILES, BASES], F32)
         c4 = const.tile([P, F_TILES, BASES], F32)
 
         def spline_constants():
-            gap = {}
-            inv = {}
-            for span in (1, 2, 3, 4):
-                count = KNOTS + 1 - span
-                gap[span] = const.tile([P, F_TILES, count], F32, name="gap%d" % span)
-                nc.vector.tensor_sub(out=gap[span][:], in0=knot[:, :, span : KNOTS + 1], in1=knot[:, :, 0:count])
-                inv[span] = const.tile([P, F_TILES, count], F32, name="inv%d" % span)
+            for span in (1, 2, 3):
+                inv[span] = const.tile([P, F_TILES, KNOTS + 1 - span], F32, name="inv%d" % span)
                 nc.vector.reciprocal(out=inv[span][:], in_=gap[span][:])
-            nc.vector.tensor_mul(out=sigma[:], in0=inv[1][:, :, 0:8], in1=inv[2][:, :, 0:8])
-            nc.vector.tensor_mul(out=sigma[:], in0=sigma[:], in1=inv[3][:, :, 0:8])
-            nc.vector.scalar_tensor_tensor(
-                out=c1[:], in0=gap[4][:, :, 0:6], scalar=-1.0, in1=inv[1][:, :, 0:6], op0=ALU.mult, op1=ALU.mult
-            )
-            nc.vector.tensor_mul(out=c2[:], in0=gap[4][:, :, 0:6], in1=inv[2][:, :, 0:6])
-            nc.vector.tensor_mul(out=c2[:], in0=c2[:], in1=inv[1][:, :, 1:7])
-            nc.vector.tensor_mul(out=c2[:], in0=c2[:], in1=gap[3][:, :, 2:8])
-            nc.vector.scalar_tensor_tensor(
-                out=c4[:], in0=inv[3][:, :, 1:7], scalar=-1.0, in1=inv[2][:, :, 2:8], op0=ALU.mult, op1=ALU.mult
-            )
-            nc.vector.tensor_mul(out=c4[:], in0=c4[:], in1=inv[1][:, :, 3:9])
-
+            nc.gpsimd.tensor_mul(out=sigma[:], in0=inv[1][:, :, 0:8], in1=inv[2][:, :, 0:8])
+            nc.gpsimd.tensor_mul(out=sigma[:], in0=sigma[:], in1=inv[3][:, :, 0:8])
+            nc.gpsimd.tensor_mul(out=c1[:], in0=gap[4][:, :, 0:6], in1=inv[1][:, :, 0:6])
+            nc.gpsimd.tensor_mul(out=c2[:], in0=gap[4][:, :, 0:6], in1=inv[2][:, :, 0:6])
+            nc.gpsimd.tensor_mul(out=c2[:], in0=c2[:], in1=inv[1][:, :, 1:7])
+            nc.gpsimd.tensor_mul(out=c2[:], in0=c2[:], in1=gap[3][:, :, 2:8])
+            nc.gpsimd.tensor_mul(out=c4[:], in0=inv[3][:, :, 1:7], in1=inv[2][:, :, 2:8])
+            nc.gpsimd.tensor_mul(out=c4[:], in0=c4[:], in1=inv[1][:, :, 3:9])
+            nc.gpsimd.tensor_scalar(out=c1[:], in0=c1[:], scalar1=-1.0, scalar2=0.0, op0=ALU.mult, op1=ALU.add)
+            nc.gpsimd.tensor_scalar(out=c4[:], in0=c4[:], scalar1=-1.0, scalar2=0.0, op0=ALU.mult, op1=ALU.add)
 
         mean_var = {}
         rstd = {}
+        var_eps = {}
+        std = {}
+        shift = {}
         z = {}
         xn = {}
         relu_xn = {}
@@ -156,34 +154,39 @@ def tile_kanlinear_pa_kernel(
             for r in range(R_TILES):
                 nc.vector.bn_stats(out=stats[:, r, :], in_=x_bf[:, c * R_TILES + r, :])
                 nc.vector.bn_aggr(out=mean_var[c][:, r, :], in_=stats[:, r, :])
+            var_eps[c] = work.tile([P, R_TILES], F32, name="var_eps")
+            nc.vector.tensor_scalar_add(out=var_eps[c][:], in0=mean_var[c][:, :, 1], scalar1=LN_EPS)
+            std[c] = work.tile([P, R_TILES], F32, name="std")
+            nc.scalar.activation(out=std[c][:], in_=var_eps[c][:], func=ACT.Sqrt)
 
-        def normalise(c):
-            var_eps = work.tile([P, R_TILES], F32, name="var_eps")
-            nc.vector.tensor_scalar_add(out=var_eps[:], in0=mean_var[c][:, :, 1], scalar1=LN_EPS)
-            std = work.tile([P, R_TILES], F32, name="std")
-            nc.scalar.activation(out=std[:], in_=var_eps[:], func=ACT.Sqrt)
+        def inverse_std(c):
             rstd0 = work.tile([P, R_TILES], F32, name="rstd0")
-            nc.vector.reciprocal(out=rstd0[:], in_=std[:])
+            nc.vector.reciprocal(out=rstd0[:], in_=std[c][:])
             newton = work.tile([P, R_TILES], F32, name="newton")
             nc.vector.tensor_mul(out=newton[:], in0=rstd0[:], in1=rstd0[:])
-            nc.vector.tensor_mul(out=newton[:], in0=newton[:], in1=var_eps[:])
+            nc.vector.tensor_mul(out=newton[:], in0=newton[:], in1=var_eps[c][:])
             nc.vector.tensor_scalar(
                 out=newton[:], in0=newton[:], scalar1=-0.5, scalar2=1.5, op0=ALU.mult, op1=ALU.add
             )
             rstd[c] = work.tile([P, R_TILES], F32, name="rstd")
             nc.vector.tensor_mul(out=rstd[c][:], in0=rstd0[:], in1=newton[:])
+            shift[c] = work.tile([P, R_TILES], F32, name="shift")
+            nc.vector.scalar_tensor_tensor(
+                out=shift[c][:], in0=mean_var[c][:, :, 0], scalar=-1.0, in1=rstd[c][:], op0=ALU.mult, op1=ALU.mult
+            )
+
+        def normalise(c):
             for r in range(R_TILES):
                 z[c, r] = work.tile([P, FEATURES], F32, name="z", bufs=ROWS // P)
-                nc.vector.tensor_scalar(
-                    out=z[c, r][:], in0=x_bf[:, c * R_TILES + r, :],
-                    scalar1=mean_var[c][:, r, 0:1], scalar2=rstd[c][:, r : r + 1],
-                    op0=ALU.subtract, op1=ALU.mult,
+                nc.scalar.activation(
+                    out=z[c, r][:], in_=x_bf[:, c * R_TILES + r, :], func=ACT.Identity,
+                    scale=rstd[c][:, r : r + 1], bias=shift[c][:, r : r + 1],
                 )
 
         def features_to_partitions(c, a):
             if a == 0:
                 relu_xn[c] = work.tile([P, F_TILES, CHUNK], BF16, name="relu_xn")
-            z_t = psum.tile([P, CHUNK], F32, name="z_t", tag="turned")
+            z_t = psum.tile([P, CHUNK], F32, name="z_t", bufs=1)
             for r in range(R_TILES):
                 nc.tensor.transpose(z_t[:, r * P : (r + 1) * P], z[c, r][:, a * P : (a + 1) * P], ident_f32[:])
             xn[c, a] = work.tile([P, CHUNK], F32, name="xn", bufs=3)
@@ -230,7 +233,7 @@ def tile_kanlinear_pa_kernel(
                     op0=ALU.mult, op1=ALU.min,
                 )
 
-        def bases_to_rows(c, a, vector_helps):
+        def bases_to_rows(c, a):
             first = FEATURES + a * P * BASES
             for r in range(R_TILES):
                 if a == 0:
@@ -238,15 +241,11 @@ def tile_kanlinear_pa_kernel(
                 back = psum.tile([P, BASES * P], BF16, name="back")
                 for j in range(BASES):
                     nc.tensor.transpose(back[:, j * P : (j + 1) * P], bases[c, a][:, j, r * P : (r + 1) * P], ident_bf[:])
-                by_feature = rows[c, r][:, first : first + P * BASES].rearrange("n (f j) -> n f j", j=BASES)
-                if vector_helps and r % 2 == 1:
-                    nc.vector.tensor_scalar_max(
-                        out=by_feature, in0=back[:].rearrange("n (j f) -> n f j", j=BASES), scalar1=0.0
-                    )
-                else:
-                    nc.scalar.activation(
-                        out=by_feature, in_=back[:].rearrange("n (j f) -> n f j", j=BASES), func=ACT.Relu
-                    )
+                nc.scalar.activation(
+                    out=rows[c, r][:, first : first + P * BASES].rearrange("n (f j) -> n f j", j=BASES),
+                    in_=back[:].rearrange("n (j f) -> n f j", j=BASES),
+                    func=ACT.Relu,
+                )
 
         def relu_to_rows(c):
             for r in range(R_TILES):
@@ -255,92 +254,89 @@ def tile_kanlinear_pa_kernel(
                     nc.tensor.transpose(back[:, a * P : (a + 1) * P], relu_xn[c][:, a, r * P : (r + 1) * P], ident_bf[:])
                 nc.scalar.copy(out=rows[c, r][:, 0:FEATURES], in_=back[:, 0:FEATURES])
 
-        def k_to_partitions(c, g, vector_helps):
+        def k_to_partitions(c, g):
             grouped[g] = work.tile([P, 4 * CHUNK], BF16, name="grouped", align_bytes=64, bufs=3)
             grouped_words = grouped[g][:].bitcast(F32).rearrange("p (n u) -> p n u", u=2)
             for pair in range(R_TILES // 2):
-                k_t = psum.tile([P, 2, 2, P], F32, name="k_t", tag="turned")
+                k_t = psum.tile([P, 2, 2, P], F32, name="k_t")
                 for rr in range(2):
                     row_words = rows[c, 2 * pair + rr][:].bitcast(F32)
                     for u in range(2):
                         nc.tensor.transpose(
                             k_t[:, rr, u, :], row_words[:, 256 * g + u : 256 * (g + 1) : 2], ident_f32[:]
                         )
-                side_by_side = grouped_words[:, 2 * pair * P : 2 * (pair + 1) * P, :].rearrange(
-                    "p (rr n) u -> p rr n u", rr=2
+                nc.scalar.copy(
+                    out=grouped_words[:, 2 * pair * P : 2 * (pair + 1) * P, :].rearrange("p (rr n) u -> p rr n u", rr=2),
+                    in_=k_t[:].rearrange("p rr u n -> p rr n u"),
                 )
-                if vector_helps and pair % 2 == 1:
-                    nc.vector.tensor_copy(out=side_by_side, in_=k_t[:].rearrange("p rr u n -> p rr n u"))
-                else:
-                    nc.scalar.copy(out=side_by_side, in_=k_t[:].rearrange("p rr u n -> p rr n u"))
 
         def quantise(c, g):
             nc.vector.quantize_mx(out=codes[c][:, g, :].bitcast(FP8X4), scales=planes[c][:, g, :], in_=grouped[g][:])
 
-        def passes_after(a):
-            first = 1 + (a * P * BASES) // K_PASS
-            last = ((a + 1) * P * BASES) // K_PASS
-            return list(range(first, last + 1)) + ([0] if a == 2 else [])
-
-        first_pass = passes_after(0)[0]
-        last_pass = passes_after(F_TILES - 1)[-1]
-
-        def multiply(c, g):
-            for r in range(R_TILES):
-                if g == first_pass:
-                    acc[r] = psum.tile([P, UNITS], F32, name="acc", bufs=R_TILES)
-                n_cols = slice(r * P, (r + 1) * P)
+        def multiply(c, r):
+            acc[r] = psum.tile([P, UNITS], F32, name="acc")
+            n_cols = slice(r * P, (r + 1) * P)
+            for g in range(PASSES):
                 nc.tensor.matmul_mx(
                     out=acc[r][:],
                     lhsT=codes[c][:, g, n_cols].bitcast(FP8X4),
                     lhsT_scale=planes[c][:, g, n_cols],
                     rhs=w_words[:, g, :].bitcast(FP8X4),
                     rhs_scale=w_planes[:, g, :],
-                    start=(g == first_pass),
-                    stop=(g == last_pass),
+                    start=(g == 0),
+                    stop=(g == PASSES - 1),
                 )
 
-        def add_bias_and_store(c):
-            for r in range(R_TILES):
-                result = work.tile([P, UNITS], F32, name="result")
-                nc.vector.tensor_add(out=result[:], in0=acc[r][:], in1=bias_bf[:])
-                row0 = (c * R_TILES + r) * P
-                nc.sync.dma_start(out=out[row0 : row0 + P, :], in_=result[:])
+        def add_bias_and_store(c, r):
+            result = work.tile([P, UNITS], F32, name="result")
+            nc.vector.tensor_add(out=result[:], in0=acc[r][:], in1=bias_bf[:])
+            row0 = (c * R_TILES + r) * P
+            nc.sync.dma_start(out=out[row0 : row0 + P, :], in_=result[:])
+
+        def passes_after(a):
+            first = 1 + (a * P * BASES) // K_PASS
+            last = ((a + 1) * P * BASES) // K_PASS
+            return list(range(first, last + 1)) + ([0] if a == 2 else [])
 
         statistics(0)
-        norm_constants()
+        inverse_std(0)
         normalise(0)
         spline_constants()
         features_to_partitions(0, 0)
         squares(0, 0)
         statistics(1)
         n_units = len(UNITS_OF_WORK)
-        for t in range(n_units + 1):
-            last_step = t == n_units
+        for t in range(n_units + 3):
             if t < n_units:
                 cubes(*UNITS_OF_WORK[t])
             ready = []
-            if t >= 1:
+            if 1 <= t <= n_units:
                 pc, pa = UNITS_OF_WORK[t - 1]
                 if pa == 0:
                     codes[pc] = work.tile([P, PASSES, CHUNK], U32, name="codes", align_bytes=64)
                     planes[pc] = work.tile([P, PASSES, CHUNK], U8, name="planes", align_bytes=64)
-                bases_to_rows(pc, pa, last_step)
+                bases_to_rows(pc, pa)
                 if pa == 2:
                     relu_to_rows(pc)
                 ready = passes_after(pa)
                 for g in ready:
-                    k_to_partitions(pc, g, last_step)
+                    k_to_partitions(pc, g)
             if t + 1 < n_units:
                 features_to_partitions(*UNITS_OF_WORK[t + 1])
                 squares(*UNITS_OF_WORK[t + 1])
+            if t == 1:
+                normalise(1)
             if t < n_units:
                 combine(*UNITS_OF_WORK[t])
             if t == 0:
-                normalise(1)
-            if t >= 1 and pa == 0 and pc >= 1:
-                add_bias_and_store(pc - 1)
+                inverse_std(1)
             for g in ready:
                 quantise(pc, g)
-                multiply(pc, g)
-        add_bias_and_store(CHUNKS - 1)
+            if t >= F_TILES:
+                done, step = divmod(t - F_TILES, F_TILES)
+                if 1 <= step <= 2:
+                    add_bias_and_store(done, 2 * step - 2)
+                    add_bias_and_store(done, 2 * step - 1)
+                if step <= 1:
+                    multiply(done, 2 * step)
+                    multiply(done, 2 * step + 1)

@@ -17,13 +17,15 @@ ROWS, FEATURES, UNITS = 1024, 512, 512
 BASES = 6
 KNOTS = 10
 LN_EPS = 0.001
-K_PASS = 512
-PASSES = (FEATURES + FEATURES * BASES) // K_PASS
-F_TILES = FEATURES // P
+GROUPS = 2
+TILES = 2 * GROUPS
+WORDS = 3
+TRUNCATED = 7
+MASKS = 3
 CHUNK = 512
 R_TILES = CHUNK // P
 CHUNKS = ROWS // CHUNK
-UNITS_OF_WORK = [(c, a) for c in range(CHUNKS) for a in range(F_TILES)]
+STEPS = [(c, a, e) for c in range(CHUNKS) for a in range(GROUPS) for e in range(2)]
 
 FLOPS = 2 * ROWS * (FEATURES + FEATURES * BASES) * UNITS
 
@@ -44,91 +46,128 @@ def tile_kanlinear_pa_kernel(
     nc = tc.nc
     with ExitStack() as stack:
         const = stack.enter_context(tc.tile_pool(name="const", bufs=1))
-        work = stack.enter_context(tc.tile_pool(name="work", bufs=2))
+        work = stack.enter_context(tc.tile_pool(name="work", bufs=1))
         psum = stack.enter_context(tc.psum_pool(name="psum", bufs=2))
         stack.enter_context(tc.manual_schedule())
 
         x_bf = const.tile([P, ROWS // P, FEATURES], BF16)
         x_rows = x.rearrange("(r p) f -> p r f", p=P)
-        for c in range(CHUNKS):
+        for r in range(R_TILES):
+            nc.sync.dma_start(out=x_bf[:, r, :], in_=x_rows[:, r, :])
+        for c in range(1, CHUNKS):
             r_range = slice(c * R_TILES, (c + 1) * R_TILES)
             nc.sync.dma_start(out=x_bf[:, r_range, :], in_=x_rows[:, r_range, :])
 
-        knots_bf = const.tile([P, F_TILES, KNOTS], BF16)
-        gamma_bf = const.tile([P, F_TILES], BF16)
-        beta_bf = const.tile([P, F_TILES], BF16)
+        knots_bf = const.tile([P, TILES, KNOTS], BF16)
+        gamma_bf = const.tile([P, TILES], BF16)
+        beta_bf = const.tile([P, TILES], BF16)
+        gamma4_bf = const.tile([P, 4], BF16)
+        beta4_bf = const.tile([P, 4], BF16)
         bias_bf = const.tile([P, UNITS], BF16)
-        with nc.allow_non_contiguous_dma(reason="small per-feature tables, one feature to a partition"):
-            nc.scalar.dma_start(out=knots_bf[:], in_=grid[0].rearrange("(a p) i -> p a i", p=P))
-            nc.scalar.dma_start(out=gamma_bf[:], in_=ln_gamma.rearrange("(a p) -> p a", p=P))
-            nc.scalar.dma_start(out=beta_bf[:], in_=ln_beta.rearrange("(a p) -> p a", p=P))
-        nc.scalar.dma_start(out=bias_bf[:], in_=base_bias.partition_broadcast(P))
+        with nc.allow_non_contiguous_dma(reason="small per-feature tables"):
+            nc.scalar.dma_start(
+                out=knots_bf[:].rearrange("p (a e) i -> p a (e i)", e=2),
+                in_=grid[0].rearrange("(a p e) i -> p a (e i)", a=GROUPS, e=2),
+            )
+            nc.scalar.dma_start(
+                out=gamma_bf[:].rearrange("p (a e) -> p a e", e=2),
+                in_=ln_gamma.rearrange("(a p e) -> p a e", a=GROUPS, e=2),
+            )
+            nc.scalar.dma_start(
+                out=beta_bf[:].rearrange("p (a e) -> p a e", e=2),
+                in_=ln_beta.rearrange("(a p e) -> p a e", a=GROUPS, e=2),
+            )
+            nc.scalar.dma_start(out=gamma4_bf[:], in_=ln_gamma.rearrange("(p t) -> p t", t=4))
+            nc.scalar.dma_start(out=beta4_bf[:], in_=ln_beta.rearrange("(p t) -> p t", t=4))
 
-        w_words = const.tile([P, PASSES, 4 * UNITS], U8, align_bytes=64)
-        w_planes = const.tile([P, PASSES, UNITS], U8, align_bytes=64)
+        w_base = const.tile([P, 4 * UNITS], U8, align_bytes=64)
+        w_words = const.tile([P, MASKS, GROUPS, WORDS, 4 * UNITS], U8, align_bytes=64)
+        w_planes = const.tile([P, 1 + GROUPS * MASKS, UNITS], U8, align_bytes=64)
         nc.vector.memset(w_planes[:].bitcast(I32), 0)
-        nc.sync.dma_start(
-            out=w_words[:, 0, :].bitcast(I32),
-            in_=base_weight_words[0].rearrange("p n t -> p (n t)").bitcast(I32),
-        )
-        nc.sync.dma_start(
-            out=w_words[:, 1:PASSES, :].bitcast(I32),
-            in_=spline_weight_words.rearrange("g p n t -> p g (n t)").bitcast(I32),
-        )
-        for quadrant in range(4):
-            live = slice(32 * quadrant, 32 * quadrant + 4)
-            scale_rows = slice(4 * quadrant, 4 * quadrant + 4)
-            nc.sync.dma_start(
-                out=w_planes[live, 0, :].bitcast(I32),
-                in_=base_weight_scales[0, scale_rows, :].bitcast(I32),
-            )
-            nc.sync.dma_start(
-                out=w_planes[live, 1:PASSES, :].bitcast(I32),
-                in_=spline_weight_scales[:, scale_rows, :].rearrange("g r n -> r g n").bitcast(I32),
-            )
-
         ident_f32 = const.tile([P, P], F32)
         make_identity(nc, ident_f32[:])
-        ident_bf = const.tile([P, P], BF16)
-        make_identity(nc, ident_bf[:])
 
-        gamma = const.tile([P, F_TILES], F32)
-        nc.gpsimd.tensor_copy(out=gamma[:], in_=gamma_bf[:])
-        beta = const.tile([P, F_TILES], F32)
-        nc.gpsimd.tensor_copy(out=beta[:], in_=beta_bf[:])
-        knot = const.tile([P, F_TILES, KNOTS + 1], F32)
-        nc.gpsimd.tensor_copy(out=knot[:, :, 0:KNOTS], in_=knots_bf[:])
-        nc.gpsimd.tensor_sub(out=knot[:, :, 10:11], in0=knot[:, :, 9:10], in1=knot[:, :, 8:9])
-        nc.gpsimd.tensor_add(out=knot[:, :, 10:11], in0=knot[:, :, 10:11], in1=knot[:, :, 9:10])
-        neg_knot = const.tile([P, F_TILES, KNOTS], F32)
-        nc.gpsimd.tensor_scalar(
-            out=neg_knot[:], in0=knot[:, :, 0:KNOTS], scalar1=-1.0, scalar2=0.0, op0=ALU.mult, op1=ALU.add
-        )
+        g = nc.gpsimd
+        gamma = const.tile([P, TILES], F32)
+        g.tensor_copy(out=gamma[:], in_=gamma_bf[:])
+        beta = const.tile([P, TILES], F32)
+        g.tensor_copy(out=beta[:], in_=beta_bf[:])
+        knot = const.tile([P, TILES, KNOTS], F32)
+        g.tensor_copy(out=knot[:], in_=knots_bf[:])
+        gamma_sq = const.tile([P, TILES], F32)
+        g.tensor_mul(out=gamma_sq[:], in0=gamma[:], in1=gamma[:])
+        gamma_safe = const.tile([P, TILES], F32)
+        g.tensor_scalar(out=gamma_safe[:], in0=gamma_sq[:], scalar1=1e-24, scalar2=1.0, op0=ALU.is_ge, op1=ALU.mult)
+        g.tensor_mul(out=gamma_safe[:], in0=gamma_safe[:], in1=gamma[:])
+        g.tensor_scalar(out=gamma_sq[:], in0=gamma_sq[:], scalar1=1e-24, scalar2=1e-12, op0=ALU.is_lt, op1=ALU.mult)
+        g.tensor_add(out=gamma_safe[:], in0=gamma_safe[:], in1=gamma_sq[:])
+        inv_gamma = const.tile([P, TILES], F32)
+        nc.vector.reciprocal(out=inv_gamma[:], in_=gamma_safe[:])
+        offset = const.tile([P, TILES, KNOTS], F32)
+        g.tensor_sub(out=offset[:], in0=beta[:].unsqueeze(2).to_broadcast([P, TILES, KNOTS]), in1=knot[:])
+        root = const.tile([P, TILES, KNOTS], F32)
+        g.tensor_mul(out=root[:], in0=offset[:], in1=inv_gamma[:].unsqueeze(2).to_broadcast([P, TILES, KNOTS]))
         gap = {}
         inv = {}
         for span in (1, 2, 3, 4):
-            count = KNOTS + 1 - span
-            gap[span] = const.tile([P, F_TILES, count], F32, name="gap%d" % span)
-            nc.gpsimd.tensor_sub(out=gap[span][:], in0=knot[:, :, span : KNOTS + 1], in1=knot[:, :, 0:count])
-        sigma = const.tile([P, F_TILES, 8], F32)
-        c1 = const.tile([P, F_TILES, BASES], F32)
-        c2 = const.tile([P, F_TILES, BASES], F32)
-        c4 = const.tile([P, F_TILES, BASES], F32)
-
-        def spline_constants():
-            for span in (1, 2, 3):
-                inv[span] = const.tile([P, F_TILES, KNOTS + 1 - span], F32, name="inv%d" % span)
+            count = KNOTS - span
+            gap[span] = const.tile([P, TILES, count], F32, name="gap%d" % span)
+            g.tensor_sub(out=gap[span][:], in0=knot[:, :, span:KNOTS], in1=knot[:, :, 0:count])
+            if span < 4:
+                inv[span] = const.tile([P, TILES, count], F32, name="inv%d" % span)
                 nc.vector.reciprocal(out=inv[span][:], in_=gap[span][:])
-            nc.gpsimd.tensor_mul(out=sigma[:], in0=inv[1][:, :, 0:8], in1=inv[2][:, :, 0:8])
-            nc.gpsimd.tensor_mul(out=sigma[:], in0=sigma[:], in1=inv[3][:, :, 0:8])
-            nc.gpsimd.tensor_mul(out=c1[:], in0=gap[4][:, :, 0:6], in1=inv[1][:, :, 0:6])
-            nc.gpsimd.tensor_mul(out=c2[:], in0=gap[4][:, :, 0:6], in1=inv[2][:, :, 0:6])
-            nc.gpsimd.tensor_mul(out=c2[:], in0=c2[:], in1=inv[1][:, :, 1:7])
-            nc.gpsimd.tensor_mul(out=c2[:], in0=c2[:], in1=gap[3][:, :, 2:8])
-            nc.gpsimd.tensor_mul(out=c4[:], in0=inv[3][:, :, 1:7], in1=inv[2][:, :, 2:8])
-            nc.gpsimd.tensor_mul(out=c4[:], in0=c4[:], in1=inv[1][:, :, 3:9])
-            nc.gpsimd.tensor_scalar(out=c1[:], in0=c1[:], scalar1=-1.0, scalar2=0.0, op0=ALU.mult, op1=ALU.add)
-            nc.gpsimd.tensor_scalar(out=c4[:], in0=c4[:], scalar1=-1.0, scalar2=0.0, op0=ALU.mult, op1=ALU.add)
+        rise = const.tile([P, TILES, TRUNCATED], F32)
+        g.tensor_mul(out=rise[:], in0=inv[1][:, :, 0:7], in1=inv[2][:, :, 0:7])
+        g.tensor_mul(out=rise[:], in0=rise[:], in1=inv[3][:, :, 0:7])
+        g.tensor_mul(out=rise[:], in0=rise[:], in1=gamma_safe[:].unsqueeze(2).to_broadcast([P, TILES, TRUNCATED]))
+        fall = const.tile([P, TILES, TRUNCATED], F32)
+        g.tensor_mul(out=fall[:], in0=inv[1][:, :, 2:9], in1=inv[2][:, :, 1:8])
+        g.tensor_mul(out=fall[:], in0=fall[:], in1=inv[3][:, :, 0:7])
+        g.tensor_scalar(out=fall[:], in0=fall[:], scalar1=-1.0, scalar2=0.0, op0=ALU.mult, op1=ALU.add)
+        g.tensor_mul(out=fall[:], in0=fall[:], in1=gamma_safe[:].unsqueeze(2).to_broadcast([P, TILES, TRUNCATED]))
+        neg_gap4 = const.tile([P, TILES, BASES], F32)
+        g.tensor_scalar(out=neg_gap4[:], in0=gap[4][:], scalar1=-1.0, scalar2=0.0, op0=ALU.mult, op1=ALU.add)
+        c_low = const.tile([P, TILES, BASES], F32)
+        g.tensor_mul(out=c_low[:], in0=neg_gap4[:], in1=inv[1][:, :, 0:6])
+        c_high = const.tile([P, TILES, BASES], F32)
+        g.tensor_mul(out=c_high[:], in0=neg_gap4[:], in1=inv[1][:, :, 3:9])
+        gamma4 = const.tile([P, 4], F32)
+        g.tensor_copy(out=gamma4[:], in_=gamma4_bf[:])
+        beta4 = const.tile([P, 4], F32)
+        g.tensor_copy(out=beta4[:], in_=beta4_bf[:])
+
+        for m in range(MASKS):
+            g.memset(w_words[:, m].rearrange("p a i c -> p (a i c)").bitcast(I32), 0)
+        nc.sync.dma_start(
+            out=w_base[:].bitcast(I32),
+            in_=base_weight_words[0].rearrange("p n t -> p (n t)").bitcast(I32),
+        )
+        scale_rows = spline_weight_scales.rearrange("g r n -> (g r) n").bitcast(I32).rearrange(
+            "(a q i m) n -> q i a (m n)", a=GROUPS, q=4, i=4
+        )
+        for quadrant in range(4):
+            live = slice(32 * quadrant, 32 * quadrant + 4)
+            nc.sync.dma_start(
+                out=w_planes[live, 0, :].bitcast(I32),
+                in_=base_weight_scales[0, 4 * quadrant : 4 * quadrant + 4, :].bitcast(I32),
+            )
+            nc.sync.dma_start(
+                out=w_planes[live, 1:, :].rearrange("i (a m) n -> i a (m n)", a=GROUPS).bitcast(I32),
+                in_=scale_rows[quadrant],
+            )
+        word_rows = spline_weight_words.rearrange("g p n t -> (g p) (n t)").bitcast(I32).rearrange(
+            "(a b u i) c -> u b a i c", a=GROUPS, u=8, i=WORDS
+        )
+        for m in range(MASKS):
+            for u in range(8):
+                words = [i for i in range(WORDS) if (3 * u + i) // 8 == m]
+                if words:
+                    run = slice(words[0], words[-1] + 1)
+                    nc.sync.dma_start(
+                        out=w_words[u:P:8, m, :, run, :].rearrange("b a i c -> b a (i c)").bitcast(I32),
+                        in_=word_rows[u][:, :, run, :].rearrange("b a i c -> b a (i c)"),
+                    )
+        nc.sync.dma_start(out=bias_bf[:], in_=base_bias.partition_broadcast(P))
 
         mean_var = {}
         rstd = {}
@@ -136,41 +175,40 @@ def tile_kanlinear_pa_kernel(
         std = {}
         shift = {}
         z = {}
-        xn = {}
-        relu_xn = {}
+        z_t = {}
         square = {}
-        cube = {}
-        pos = {}
-        bases = {}
-        rows = {}
-        grouped = {}
         codes = {}
         planes = {}
         acc = {}
+        pos = {}
+        neg = {}
+        left = const.tile([P, 2 * BASES, CHUNK], F32)
+        right = const.tile([P, 2 * BASES, CHUNK], F32)
 
         def statistics(c):
-            stats = work.tile([P, R_TILES, 6], F32, name="stats")
-            mean_var[c] = work.tile([P, R_TILES, 2], F32, name="mean_var")
+            stats = work.tile([P, R_TILES, 6], F32, name="stats", bufs=2)
+            mean_var[c] = work.tile([P, R_TILES, 2], F32, name="mean_var", bufs=2)
             for r in range(R_TILES):
                 nc.vector.bn_stats(out=stats[:, r, :], in_=x_bf[:, c * R_TILES + r, :])
+            for r in range(R_TILES):
                 nc.vector.bn_aggr(out=mean_var[c][:, r, :], in_=stats[:, r, :])
-            var_eps[c] = work.tile([P, R_TILES], F32, name="var_eps")
+            var_eps[c] = work.tile([P, R_TILES], F32, name="var_eps", bufs=2)
             nc.vector.tensor_scalar_add(out=var_eps[c][:], in0=mean_var[c][:, :, 1], scalar1=LN_EPS)
-            std[c] = work.tile([P, R_TILES], F32, name="std")
+            std[c] = work.tile([P, R_TILES], F32, name="std", bufs=2)
             nc.scalar.activation(out=std[c][:], in_=var_eps[c][:], func=ACT.Sqrt)
 
         def inverse_std(c):
-            rstd0 = work.tile([P, R_TILES], F32, name="rstd0")
+            rstd0 = work.tile([P, R_TILES], F32, name="rstd0", bufs=2)
             nc.vector.reciprocal(out=rstd0[:], in_=std[c][:])
-            newton = work.tile([P, R_TILES], F32, name="newton")
+            newton = work.tile([P, R_TILES], F32, name="newton", bufs=2)
             nc.vector.tensor_mul(out=newton[:], in0=rstd0[:], in1=rstd0[:])
             nc.vector.tensor_mul(out=newton[:], in0=newton[:], in1=var_eps[c][:])
             nc.vector.tensor_scalar(
                 out=newton[:], in0=newton[:], scalar1=-0.5, scalar2=1.5, op0=ALU.mult, op1=ALU.add
             )
-            rstd[c] = work.tile([P, R_TILES], F32, name="rstd")
+            rstd[c] = work.tile([P, R_TILES], F32, name="rstd", bufs=2)
             nc.vector.tensor_mul(out=rstd[c][:], in0=rstd0[:], in1=newton[:])
-            shift[c] = work.tile([P, R_TILES], F32, name="shift")
+            shift[c] = work.tile([P, R_TILES], F32, name="shift", bufs=2)
             nc.vector.scalar_tensor_tensor(
                 out=shift[c][:], in0=mean_var[c][:, :, 0], scalar=-1.0, in1=rstd[c][:], op0=ALU.mult, op1=ALU.mult
             )
@@ -178,165 +216,180 @@ def tile_kanlinear_pa_kernel(
         def normalise(c):
             for r in range(R_TILES):
                 z[c, r] = work.tile([P, FEATURES], F32, name="z", bufs=ROWS // P)
-                nc.scalar.activation(
-                    out=z[c, r][:], in_=x_bf[:, c * R_TILES + r, :], func=ACT.Identity,
-                    scale=rstd[c][:, r : r + 1], bias=shift[c][:, r : r + 1],
+                nc.vector.tensor_scalar(
+                    out=z[c, r][:], in0=x_bf[:, c * R_TILES + r, :], scalar1=rstd[c][:, r : r + 1],
+                    scalar2=shift[c][:, r : r + 1], op0=ALU.mult, op1=ALU.add,
                 )
 
-        def features_to_partitions(c, a):
-            if a == 0:
-                relu_xn[c] = work.tile([P, F_TILES, CHUNK], BF16, name="relu_xn")
-            z_t = psum.tile([P, CHUNK], F32, name="z_t", bufs=1)
+        def features_to_partitions(c, a, e):
+            z_t[c, a, e] = psum.tile([P, CHUNK], F32, name="z_t")
             for r in range(R_TILES):
-                nc.tensor.transpose(z_t[:, r * P : (r + 1) * P], z[c, r][:, a * P : (a + 1) * P], ident_f32[:])
-            xn[c, a] = work.tile([P, CHUNK], F32, name="xn", bufs=3)
-            nc.scalar.activation(
-                out=xn[c, a][:], in_=z_t[:], func=ACT.Identity, scale=gamma[:, a : a + 1], bias=beta[:, a : a + 1]
-            )
-            nc.scalar.activation(
-                out=relu_xn[c][:, a, :], in_=z_t[:], func=ACT.Relu, scale=gamma[:, a : a + 1], bias=beta[:, a : a + 1]
-            )
+                nc.tensor.transpose(
+                    z_t[c, a, e][:, r * P : (r + 1) * P], z[c, r][:, 256 * a + e : 256 * (a + 1) : 2], ident_f32[:]
+                )
 
-        def squares(c, a):
+        def squares(c, a, e):
+            q = 2 * a + e
             for i in range(KNOTS):
-                square[i] = work.tile([P, CHUNK], F32, name="square%d" % i, bufs=1)
-                nc.scalar.activation(out=square[i][:], in_=xn[c, a][:], func=ACT.Square, bias=neg_knot[:, a, i : i + 1])
-
-        def cubes(c, a):
-            for i in range(KNOTS):
-                cube[i] = work.tile([P, CHUNK], F32, name="cube%d" % i, bufs=1)
-                nc.vector.scalar_tensor_tensor(
-                    out=cube[i][:], in0=xn[c, a][:], scalar=knot[:, a, i : i + 1], in1=square[i][:],
-                    op0=ALU.subtract, op1=ALU.mult,
-                )
-                if i < 8:
-                    pos[i] = work.tile([P, CHUNK], F32, name="pos%d" % i, bufs=1)
-                    nc.scalar.activation(out=pos[i][:], in_=cube[i][:], func=ACT.Relu, scale=sigma[:, a, i : i + 1])
-
-        def combine(c, a):
-            left = {}
-            for j in range(BASES):
-                left[j] = work.tile([P, CHUNK], F32, name="left%d" % j, bufs=1)
-                nc.vector.scalar_tensor_tensor(
-                    out=left[j][:], in0=pos[j + 2][:], scalar=c2[:, a, j : j + 1], in1=pos[j][:],
-                    op0=ALU.mult, op1=ALU.add,
-                )
-            for j in range(BASES):
-                nc.vector.scalar_tensor_tensor(
-                    out=left[j][:], in0=pos[j + 1][:], scalar=c1[:, a, j : j + 1], in1=left[j][:],
-                    op0=ALU.mult, op1=ALU.add,
-                )
-            bases[c, a] = work.tile([P, BASES, CHUNK], BF16, name="bases", bufs=2)
-            for j in range(BASES):
-                nc.vector.scalar_tensor_tensor(
-                    out=bases[c, a][:, j, :], in0=cube[j + 4][:], scalar=c4[:, a, j : j + 1], in1=left[j][:],
-                    op0=ALU.mult, op1=ALU.min,
-                )
-
-        def bases_to_rows(c, a):
-            first = FEATURES + a * P * BASES
-            for r in range(R_TILES):
-                if a == 0:
-                    rows[c, r] = work.tile([P, PASSES * K_PASS], BF16, name="rows", bufs=R_TILES)
-                back = psum.tile([P, BASES * P], BF16, name="back")
-                for j in range(BASES):
-                    nc.tensor.transpose(back[:, j * P : (j + 1) * P], bases[c, a][:, j, r * P : (r + 1) * P], ident_bf[:])
+                square[i] = work.tile([P, CHUNK], F32, name="square%d" % i)
                 nc.scalar.activation(
-                    out=rows[c, r][:, first : first + P * BASES].rearrange("n (f j) -> n f j", j=BASES),
-                    in_=back[:].rearrange("n (j f) -> n f j", j=BASES),
-                    func=ACT.Relu,
+                    out=square[i][:], in_=z_t[c, a, e][:], func=ACT.Square,
+                    scale=gamma[:, q : q + 1], bias=offset[:, q, i : i + 1],
                 )
 
-        def relu_to_rows(c):
+        def cubes(c, a, e):
+            q = 2 * a + e
+            for i in range(KNOTS):
+                cube = work.tile([P, CHUNK], F32, name="cube", bufs=4)
+                nc.vector.scalar_tensor_tensor(
+                    out=cube[:], in0=z_t[c, a, e][:], scalar=root[:, q, i : i + 1], in1=square[i][:],
+                    op0=ALU.add, op1=ALU.mult,
+                )
+                if i < TRUNCATED:
+                    pos[i] = work.tile([P, CHUNK], F32, name="pos%d" % i)
+                    nc.scalar.activation(out=pos[i][:], in_=cube[:], func=ACT.Relu, scale=rise[:, q, i : i + 1])
+                if i >= 3:
+                    neg[i] = work.tile([P, CHUNK], F32, name="neg%d" % i)
+                    nc.scalar.activation(out=neg[i][:], in_=cube[:], func=ACT.Relu, scale=fall[:, q, i - 3 : i - 2])
+
+        def left_side(a, e, j):
+            nc.vector.scalar_tensor_tensor(
+                out=left[:, BASES * e + j, :], in0=pos[j + 1][:], scalar=c_low[:, 2 * a + e, j : j + 1],
+                in1=pos[j][:], op0=ALU.mult, op1=ALU.add,
+            )
+
+        def right_side(a, e, j):
+            nc.vector.scalar_tensor_tensor(
+                out=right[:, BASES * e + j, :], in0=neg[j + 3][:], scalar=c_high[:, 2 * a + e, j : j + 1],
+                in1=neg[j + 4][:], op0=ALU.mult, op1=ALU.add,
+            )
+
+        def relu_branch(c):
+            flat = work.tile([P, 4, CHUNK], BF16, name="relu_flat")
+            for t in range(4):
+                z_r = psum.tile([P, CHUNK], F32, name="z_r")
+                for r in range(R_TILES):
+                    nc.tensor.transpose(z_r[:, r * P : (r + 1) * P], z[c, r][:, t::4], ident_f32[:])
+                nc.scalar.activation(
+                    out=flat[:, t, :], in_=z_r[:], func=ACT.Relu, scale=gamma4[:, t : t + 1], bias=beta4[:, t : t + 1]
+                )
+            return flat
+
+        def interleave_relu(flat):
+            relu_grouped = work.tile([P, 4 * CHUNK], BF16, name="relu_grouped", align_bytes=64)
+            nc.vector.tensor_copy(
+                out=relu_grouped[:].rearrange("p (c i t) -> p c t i", i=4, t=4),
+                in_=flat[:].rearrange("p t (c i) -> p c t i", i=4),
+            )
+            return relu_grouped
+
+        def finish_words(i):
+            words = work.tile([P, 4 * CHUNK], BF16, name="words", align_bytes=64, bufs=3)
+            four = slice(4 * i, 4 * i + 4)
+            nc.vector.tensor_tensor(
+                out=words[:].rearrange("p (c i t) -> p c t i", i=4, t=4),
+                in0=left[:, four, :].rearrange("p t (c i) -> p c t i", i=4),
+                in1=right[:, four, :].rearrange("p t (c i) -> p c t i", i=4),
+                op=ALU.max,
+            )
+            return words
+
+        def quantise(c, slot, source):
+            nc.vector.quantize_mx(
+                out=codes[c][:, slot, :].bitcast(FP8X4), scales=planes[c][:, slot, :], in_=source[:]
+            )
+
+        def multiply(c, slot, weights, plane, start, stop):
             for r in range(R_TILES):
-                back = psum.tile([P, BASES * P], BF16, name="back")
-                for a in range(F_TILES):
-                    nc.tensor.transpose(back[:, a * P : (a + 1) * P], relu_xn[c][:, a, r * P : (r + 1) * P], ident_bf[:])
-                nc.scalar.copy(out=rows[c, r][:, 0:FEATURES], in_=back[:, 0:FEATURES])
-
-        def k_to_partitions(c, g):
-            grouped[g] = work.tile([P, 4 * CHUNK], BF16, name="grouped", align_bytes=64, bufs=3)
-            grouped_words = grouped[g][:].bitcast(F32).rearrange("p (n u) -> p n u", u=2)
-            for pair in range(R_TILES // 2):
-                k_t = psum.tile([P, 2, 2, P], F32, name="k_t")
-                for rr in range(2):
-                    row_words = rows[c, 2 * pair + rr][:].bitcast(F32)
-                    for u in range(2):
-                        nc.tensor.transpose(
-                            k_t[:, rr, u, :], row_words[:, 256 * g + u : 256 * (g + 1) : 2], ident_f32[:]
-                        )
-                nc.scalar.copy(
-                    out=grouped_words[:, 2 * pair * P : 2 * (pair + 1) * P, :].rearrange("p (rr n) u -> p rr n u", rr=2),
-                    in_=k_t[:].rearrange("p rr u n -> p rr n u"),
-                )
-
-        def quantise(c, g):
-            nc.vector.quantize_mx(out=codes[c][:, g, :].bitcast(FP8X4), scales=planes[c][:, g, :], in_=grouped[g][:])
-
-        def multiply(c, r):
-            acc[r] = psum.tile([P, UNITS], F32, name="acc")
-            n_cols = slice(r * P, (r + 1) * P)
-            for g in range(PASSES):
+                n_cols = slice(r * P, (r + 1) * P)
                 nc.tensor.matmul_mx(
-                    out=acc[r][:],
-                    lhsT=codes[c][:, g, n_cols].bitcast(FP8X4),
-                    lhsT_scale=planes[c][:, g, n_cols],
-                    rhs=w_words[:, g, :].bitcast(FP8X4),
-                    rhs_scale=w_planes[:, g, :],
-                    start=(g == 0),
-                    stop=(g == PASSES - 1),
+                    out=acc[c, r][:],
+                    lhsT=codes[c][:, slot, n_cols].bitcast(FP8X4),
+                    lhsT_scale=planes[c][:, slot, n_cols],
+                    rhs=weights.bitcast(FP8X4),
+                    rhs_scale=w_planes[:, plane, :],
+                    start=start,
+                    stop=stop,
                 )
 
-        def add_bias_and_store(c, r):
-            result = work.tile([P, UNITS], F32, name="result")
-            nc.vector.tensor_add(out=result[:], in0=acc[r][:], in1=bias_bf[:])
-            row0 = (c * R_TILES + r) * P
-            nc.sync.dma_start(out=out[row0 : row0 + P, :], in_=result[:])
+        def multiply_words(c, a, i):
+            for m in range(MASKS):
+                multiply(
+                    c, 1 + WORDS * a + i, w_words[:, m, a, i, :], 1 + MASKS * a + m,
+                    start=(a == 0 and i == 0 and m == 0),
+                    stop=(a == GROUPS - 1 and i == WORDS - 1 and m == MASKS - 1),
+                )
 
-        def passes_after(a):
-            first = 1 + (a * P * BASES) // K_PASS
-            last = ((a + 1) * P * BASES) // K_PASS
-            return list(range(first, last + 1)) + ([0] if a == 2 else [])
+        def add_bias_and_store(c):
+            for r in range(R_TILES):
+                result = work.tile([P, UNITS], F32, name="result", bufs=3)
+                nc.vector.tensor_add(out=result[:], in0=acc[c, r][:], in1=bias_bf[:])
+                row0 = (c * R_TILES + r) * P
+                nc.sync.dma_start(out=out[row0 : row0 + P, :], in_=result[:])
 
         statistics(0)
         inverse_std(0)
         normalise(0)
-        spline_constants()
-        features_to_partitions(0, 0)
-        squares(0, 0)
+        features_to_partitions(*STEPS[0])
+        squares(*STEPS[0])
         statistics(1)
-        n_units = len(UNITS_OF_WORK)
-        for t in range(n_units + 3):
-            if t < n_units:
-                cubes(*UNITS_OF_WORK[t])
-            ready = []
-            if 1 <= t <= n_units:
-                pc, pa = UNITS_OF_WORK[t - 1]
-                if pa == 0:
-                    codes[pc] = work.tile([P, PASSES, CHUNK], U32, name="codes", align_bytes=64)
-                    planes[pc] = work.tile([P, PASSES, CHUNK], U8, name="planes", align_bytes=64)
-                bases_to_rows(pc, pa)
-                if pa == 2:
-                    relu_to_rows(pc)
-                ready = passes_after(pa)
-                for g in ready:
-                    k_to_partitions(pc, g)
-            if t + 1 < n_units:
-                features_to_partitions(*UNITS_OF_WORK[t + 1])
-                squares(*UNITS_OF_WORK[t + 1])
+        inverse_std(1)
+        words = {}
+        flat = {}
+        for t, (c, a, e) in enumerate(STEPS):
+            last = t == len(STEPS) - 1
+            if a == 0 and e == 0:
+                codes[c] = work.tile([P, 1 + GROUPS * WORDS, CHUNK], U32, name="codes", align_bytes=64, bufs=2)
+                planes[c] = work.tile([P, 1 + GROUPS * WORDS, CHUNK], U8, name="planes", align_bytes=64, bufs=2)
+            if not last:
+                features_to_partitions(*STEPS[t + 1])
+            cubes(c, a, e)
+            if a == 0 and e == 1 and c > 0:
+                add_bias_and_store(c - 1)
+            if not last:
+                squares(*STEPS[t + 1])
+            if a == 0 and e == 1:
+                flat[c] = relu_branch(c)
             if t == 1:
                 normalise(1)
-            if t < n_units:
-                combine(*UNITS_OF_WORK[t])
-            if t == 0:
-                inverse_std(1)
-            for g in ready:
-                quantise(pc, g)
-            if t >= F_TILES:
-                done, step = divmod(t - F_TILES, F_TILES)
-                if 1 <= step <= 2:
-                    add_bias_and_store(done, 2 * step - 2)
-                    add_bias_and_store(done, 2 * step - 1)
-                if step <= 1:
-                    multiply(done, 2 * step)
-                    multiply(done, 2 * step + 1)
+            left_side(a, e, 0)
+            if e == 0:
+                if t > 0:
+                    pc, pa, pe = STEPS[t - 1]
+                    quantise(pc, WORDS * (pa + 1), words[2])
+                for j in (1, 2, 3, 4, 5):
+                    left_side(a, e, j)
+                if a == 1:
+                    relu_words = interleave_relu(flat[c])
+                for j in (4, 5, 0, 1, 2):
+                    right_side(a, e, j)
+                if a == 1:
+                    quantise(c, 0, relu_words)
+                right_side(a, e, 3)
+                words[0] = finish_words(0)
+                if t > 0:
+                    multiply_words(pc, pa, 2)
+                if a == 1:
+                    multiply(c, 0, w_base[:], 0, start=False, stop=False)
+            else:
+                quantise(c, 1 + WORDS * a, words[0])
+                left_side(a, e, 1)
+                right_side(a, e, 0)
+                right_side(a, e, 1)
+                left_side(a, e, 2)
+                words[1] = finish_words(1)
+                for j in (3, 4, 5):
+                    left_side(a, e, j)
+                right_side(a, e, 2)
+                quantise(c, 2 + WORDS * a, words[1])
+                for j in (3, 4, 5):
+                    right_side(a, e, j)
+                words[2] = finish_words(2)
+                if a == 0:
+                    for r in range(R_TILES):
+                        acc[c, r] = psum.tile([P, UNITS], F32, name="acc", bufs=R_TILES)
+                multiply_words(c, a, 0)
+                multiply_words(c, a, 1)
+        quantise(CHUNKS - 1, GROUPS * WORDS, words[2])
+        multiply_words(CHUNKS - 1, GROUPS - 1, 2)
+        add_bias_and_store(CHUNKS - 1)

@@ -182,8 +182,8 @@ def tile_kanlinear_pa_kernel(
         acc = {}
         pos = {}
         neg = {}
-        left = const.tile([P, 2 * BASES, CHUNK], F32)
-        right = const.tile([P, 2 * BASES, CHUNK], F32)
+        left = const.tile([P, 2 * BASES, CHUNK], BF16)
+        right = const.tile([P, 2 * BASES, CHUNK], BF16)
 
         def statistics(c):
             stats = work.tile([P, R_TILES, 6], F32, name="stats", bufs=2)
@@ -237,9 +237,9 @@ def tile_kanlinear_pa_kernel(
                     scale=gamma[:, q : q + 1], bias=offset[:, q, i : i + 1],
                 )
 
-        def cubes(c, a, e):
+        def cubes(c, a, e, first, end):
             q = 2 * a + e
-            for i in range(KNOTS):
+            for i in range(first, end):
                 cube = work.tile([P, CHUNK], F32, name="cube", bufs=4)
                 nc.vector.scalar_tensor_tensor(
                     out=cube[:], in0=z_t[c, a, e][:], scalar=root[:, q, i : i + 1], in1=square[i][:],
@@ -275,22 +275,18 @@ def tile_kanlinear_pa_kernel(
                 )
             return flat
 
-        def interleave_relu(flat):
-            relu_grouped = work.tile([P, 4 * CHUNK], BF16, name="relu_grouped", align_bytes=64)
-            nc.vector.tensor_copy(
-                out=relu_grouped[:].rearrange("p (c i t) -> p c t i", i=4, t=4),
-                in_=flat[:].rearrange("p t (c i) -> p c t i", i=4),
-            )
-            return relu_grouped
-
-        def finish_words(i):
-            words = work.tile([P, 4 * CHUNK], BF16, name="words", align_bytes=64, bufs=3)
-            four = slice(4 * i, 4 * i + 4)
+        def larger(source, first, end):
+            slots = slice(first, end)
             nc.vector.tensor_tensor(
-                out=words[:].rearrange("p (c i t) -> p c t i", i=4, t=4),
-                in0=left[:, four, :].rearrange("p t (c i) -> p c t i", i=4),
-                in1=right[:, four, :].rearrange("p t (c i) -> p c t i", i=4),
-                op=ALU.max,
+                out=source[:, slots, :], in0=left[:, slots, :], in1=right[:, slots, :], op=ALU.max
+            )
+
+        def interleave(engine, source, first):
+            words = work.tile([P, 4 * CHUNK], BF16, name="words", align_bytes=64, bufs=4)
+            engine.tensor_scalar(
+                out=words[:].rearrange("p (n t) -> p n t", t=4),
+                in0=source[:, first : first + 4, :].rearrange("p t n -> p n t"),
+                scalar1=1.0, scalar2=0.0, op0=ALU.mult, op1=ALU.add,
             )
             return words
 
@@ -336,6 +332,7 @@ def tile_kanlinear_pa_kernel(
         inverse_std(1)
         words = {}
         flat = {}
+        bases = {}
         for t, (c, a, e) in enumerate(STEPS):
             last = t == len(STEPS) - 1
             if a == 0 and e == 0:
@@ -343,7 +340,19 @@ def tile_kanlinear_pa_kernel(
                 planes[c] = work.tile([P, 1 + GROUPS * WORDS, CHUNK], U8, name="planes", align_bytes=64, bufs=2)
             if not last:
                 features_to_partitions(*STEPS[t + 1])
-            cubes(c, a, e)
+            cubes(c, a, e, 0, 1)
+            if e == 0:
+                if t > 0:
+                    pc, pa, pe = STEPS[t - 1]
+                    larger(bases[pc, pa], 4, 12)
+                    for i in (1, 2):
+                        words[i] = interleave(nc.gpsimd, bases[pc, pa], 4 * i)
+                bases[c, a] = work.tile([P, 2 * BASES, CHUNK], BF16, name="bases", bufs=2)
+            else:
+                words[0] = interleave(nc.gpsimd, bases[c, a], 0)
+                if a == 1:
+                    relu_words = interleave(nc.gpsimd, flat[c], 0)
+            cubes(c, a, e, 1, KNOTS)
             if a == 0 and e == 1 and c > 0:
                 add_bias_and_store(c - 1)
             if not last:
@@ -352,44 +361,51 @@ def tile_kanlinear_pa_kernel(
                 flat[c] = relu_branch(c)
             if t == 1:
                 normalise(1)
-            left_side(a, e, 0)
             if e == 0:
+                left_side(a, e, 0)
                 if t > 0:
-                    pc, pa, pe = STEPS[t - 1]
-                    quantise(pc, WORDS * (pa + 1), words[2])
-                for j in (1, 2, 3, 4, 5):
+                    quantise(pc, WORDS * pa + 2, words[1])
+                left_side(a, e, 1)
+                if t > 0:
+                    quantise(pc, WORDS * pa + 3, words[2])
+                for j in (2, 3, 4, 5):
                     left_side(a, e, j)
-                if a == 1:
-                    relu_words = interleave_relu(flat[c])
-                for j in (4, 5, 0, 1, 2):
+                for j in range(BASES):
                     right_side(a, e, j)
-                if a == 1:
-                    quantise(c, 0, relu_words)
-                right_side(a, e, 3)
-                words[0] = finish_words(0)
+                larger(bases[c, a], 0, 4)
                 if t > 0:
+                    multiply_words(pc, pa, 1)
                     multiply_words(pc, pa, 2)
-                if a == 1:
-                    multiply(c, 0, w_base[:], 0, start=False, stop=False)
             else:
+                left_side(a, e, 0)
                 quantise(c, 1 + WORDS * a, words[0])
                 left_side(a, e, 1)
+                if a == 1:
+                    quantise(c, 0, relu_words)
                 right_side(a, e, 0)
                 right_side(a, e, 1)
                 left_side(a, e, 2)
-                words[1] = finish_words(1)
+                if last:
+                    larger(bases[c, a], 4, 8)
                 for j in (3, 4, 5):
                     left_side(a, e, j)
+                if last:
+                    words[1] = interleave(nc.vector, bases[c, a], 4)
                 right_side(a, e, 2)
-                quantise(c, 2 + WORDS * a, words[1])
-                for j in (3, 4, 5):
-                    right_side(a, e, j)
-                words[2] = finish_words(2)
+                right_side(a, e, 3)
+                if last:
+                    quantise(c, WORDS * a + 2, words[1])
+                right_side(a, e, 4)
+                right_side(a, e, 5)
                 if a == 0:
                     for r in range(R_TILES):
                         acc[c, r] = psum.tile([P, UNITS], F32, name="acc", bufs=R_TILES)
                 multiply_words(c, a, 0)
-                multiply_words(c, a, 1)
-        quantise(CHUNKS - 1, GROUPS * WORDS, words[2])
-        multiply_words(CHUNKS - 1, GROUPS - 1, 2)
-        add_bias_and_store(CHUNKS - 1)
+                if a == 1:
+                    multiply(c, 0, w_base[:], 0, start=False, stop=False)
+        multiply_words(c, a, 1)
+        larger(bases[c, a], 8, 12)
+        words[2] = interleave(nc.vector, bases[c, a], 8)
+        quantise(c, WORDS * a + 3, words[2])
+        multiply_words(c, a, 2)
+        add_bias_and_store(c)

@@ -87,6 +87,56 @@ def tile_kanlinear_pa_kernel(
         ident_f32 = const.tile([P, P], F32)
         make_identity(nc, ident_f32[:])
 
+        stats = {}
+        mean_var = {}
+        var_eps = {}
+        rstd0 = {}
+        rstd = {}
+        z = {}
+        for c in range(CHUNKS):
+            stats[c] = const.tile([P, R_TILES, 6], F32, name="stats%d" % c)
+            mean_var[c] = const.tile([P, R_TILES, 2], F32, name="mean_var%d" % c)
+            var_eps[c] = const.tile([P, R_TILES], F32, name="var_eps%d" % c)
+
+        def row_statistics(c, tiles):
+            for r in tiles:
+                nc.vector.bn_stats(out=stats[c][:, r, :], in_=x_bf[:, c * R_TILES + r, :])
+
+        def mean_and_variance(c):
+            for r in range(R_TILES):
+                nc.vector.bn_aggr(out=mean_var[c][:, r, :], in_=stats[c][:, r, :])
+            nc.vector.tensor_scalar_add(out=var_eps[c][:], in0=mean_var[c][:, :, 1], scalar1=LN_EPS)
+
+        def rough_rstd(c):
+            rstd0[c] = work.tile([P, R_TILES], F32, name="rstd0", bufs=2)
+            nc.scalar.activation(out=rstd0[c][:], in_=var_eps[c][:], func=ACT.Abs_reciprocal_sqrt)
+
+        def fine_rstd(c):
+            newton = work.tile([P, R_TILES], F32, name="newton", bufs=2)
+            nc.vector.scalar_tensor_tensor(
+                out=newton[:], in0=rstd0[c][:], scalar=-0.5, in1=rstd0[c][:], op0=ALU.mult, op1=ALU.mult
+            )
+            nc.vector.tensor_mul(out=newton[:], in0=newton[:], in1=var_eps[c][:])
+            rstd[c] = work.tile([P, R_TILES], F32, name="rstd", bufs=2)
+            nc.vector.scalar_tensor_tensor(
+                out=rstd[c][:], in0=newton[:], scalar=1.5, in1=rstd0[c][:], op0=ALU.add, op1=ALU.mult
+            )
+
+        def normalise(c):
+            for r in range(R_TILES):
+                z[c, r] = work.tile([P, FEATURES], F32, name="z", bufs=ROWS // P)
+                nc.vector.tensor_scalar(
+                    out=z[c, r][:], in0=x_bf[:, c * R_TILES + r, :], scalar1=mean_var[c][:, r, 0:1],
+                    scalar2=rstd[c][:, r : r + 1], op0=ALU.subtract, op1=ALU.mult,
+                )
+
+        row_statistics(0, range(R_TILES))
+        mean_and_variance(0)
+        rough_rstd(0)
+        row_statistics(1, [0])
+        fine_rstd(0)
+        normalise(0)
+
         g = nc.gpsimd
         gamma = const.tile([P, TILES], F32)
         g.tensor_copy(out=gamma[:], in_=gamma_bf[:])
@@ -169,13 +219,8 @@ def tile_kanlinear_pa_kernel(
                     )
         nc.sync.dma_start(out=bias_bf[:], in_=base_bias.partition_broadcast(P))
 
-        mean_var = {}
-        rstd = {}
-        var_eps = {}
-        std = {}
-        shift = {}
-        z = {}
-        z_t = {}
+        z_s = {}
+        z_v = {}
         square = {}
         codes = {}
         planes = {}
@@ -185,64 +230,30 @@ def tile_kanlinear_pa_kernel(
         left = const.tile([P, 2 * BASES, CHUNK], BF16)
         right = const.tile([P, 2 * BASES, CHUNK], BF16)
 
-        def statistics(c):
-            stats = work.tile([P, R_TILES, 6], F32, name="stats", bufs=2)
-            mean_var[c] = work.tile([P, R_TILES, 2], F32, name="mean_var", bufs=2)
-            for r in range(R_TILES):
-                nc.vector.bn_stats(out=stats[:, r, :], in_=x_bf[:, c * R_TILES + r, :])
-            for r in range(R_TILES):
-                nc.vector.bn_aggr(out=mean_var[c][:, r, :], in_=stats[:, r, :])
-            var_eps[c] = work.tile([P, R_TILES], F32, name="var_eps", bufs=2)
-            nc.vector.tensor_scalar_add(out=var_eps[c][:], in0=mean_var[c][:, :, 1], scalar1=LN_EPS)
-            std[c] = work.tile([P, R_TILES], F32, name="std", bufs=2)
-            nc.scalar.activation(out=std[c][:], in_=var_eps[c][:], func=ACT.Sqrt)
-
-        def inverse_std(c):
-            rstd0 = work.tile([P, R_TILES], F32, name="rstd0", bufs=2)
-            nc.vector.reciprocal(out=rstd0[:], in_=std[c][:])
-            newton = work.tile([P, R_TILES], F32, name="newton", bufs=2)
-            nc.vector.tensor_mul(out=newton[:], in0=rstd0[:], in1=rstd0[:])
-            nc.vector.tensor_mul(out=newton[:], in0=newton[:], in1=var_eps[c][:])
-            nc.vector.tensor_scalar(
-                out=newton[:], in0=newton[:], scalar1=-0.5, scalar2=1.5, op0=ALU.mult, op1=ALU.add
-            )
-            rstd[c] = work.tile([P, R_TILES], F32, name="rstd", bufs=2)
-            nc.vector.tensor_mul(out=rstd[c][:], in0=rstd0[:], in1=newton[:])
-            shift[c] = work.tile([P, R_TILES], F32, name="shift", bufs=2)
-            nc.vector.scalar_tensor_tensor(
-                out=shift[c][:], in0=mean_var[c][:, :, 0], scalar=-1.0, in1=rstd[c][:], op0=ALU.mult, op1=ALU.mult
-            )
-
-        def normalise(c):
-            for r in range(R_TILES):
-                z[c, r] = work.tile([P, FEATURES], F32, name="z", bufs=ROWS // P)
-                nc.vector.tensor_scalar(
-                    out=z[c, r][:], in0=x_bf[:, c * R_TILES + r, :], scalar1=rstd[c][:, r : r + 1],
-                    scalar2=shift[c][:, r : r + 1], op0=ALU.mult, op1=ALU.add,
-                )
-
         def features_to_partitions(c, a, e):
-            z_t[c, a, e] = psum.tile([P, CHUNK], F32, name="z_t")
-            for r in range(R_TILES):
-                nc.tensor.transpose(
-                    z_t[c, a, e][:, r * P : (r + 1) * P], z[c, r][:, 256 * a + e : 256 * (a + 1) : 2], ident_f32[:]
-                )
+            z_s[c, a, e] = psum.tile([P, CHUNK], F32, name="z_s", bufs=1)
+            z_v[c, a, e] = psum.tile([P, CHUNK], F32, name="z_v", bufs=2)
+            for z_t in (z_s[c, a, e], z_v[c, a, e]):
+                for r in range(R_TILES):
+                    nc.tensor.transpose(
+                        z_t[:, r * P : (r + 1) * P], z[c, r][:, 256 * a + e : 256 * (a + 1) : 2], ident_f32[:]
+                    )
 
-        def squares(c, a, e):
+        def squares(c, a, e, first=0, end=KNOTS):
             q = 2 * a + e
-            for i in range(KNOTS):
+            for i in range(first, end):
                 square[i] = work.tile([P, CHUNK], F32, name="square%d" % i)
                 nc.scalar.activation(
-                    out=square[i][:], in_=z_t[c, a, e][:], func=ACT.Square,
+                    out=square[i][:], in_=z_s[c, a, e][:], func=ACT.Square,
                     scale=gamma[:, q : q + 1], bias=offset[:, q, i : i + 1],
                 )
 
         def cubes(c, a, e, first, end):
             q = 2 * a + e
             for i in range(first, end):
-                cube = work.tile([P, CHUNK], F32, name="cube", bufs=4)
+                cube = work.tile([P, CHUNK], F32, name="cube", bufs=8)
                 nc.vector.scalar_tensor_tensor(
-                    out=cube[:], in0=z_t[c, a, e][:], scalar=root[:, q, i : i + 1], in1=square[i][:],
+                    out=cube[:], in0=z_v[c, a, e][:], scalar=root[:, q, i : i + 1], in1=square[i][:],
                     op0=ALU.add, op1=ALU.mult,
                 )
                 if i < TRUNCATED:
@@ -264,16 +275,13 @@ def tile_kanlinear_pa_kernel(
                 in1=neg[j + 4][:], op0=ALU.mult, op1=ALU.add,
             )
 
-        def relu_branch(c):
-            flat = work.tile([P, 4, CHUNK], BF16, name="relu_flat")
-            for t in range(4):
-                z_r = psum.tile([P, CHUNK], F32, name="z_r")
-                for r in range(R_TILES):
-                    nc.tensor.transpose(z_r[:, r * P : (r + 1) * P], z[c, r][:, t::4], ident_f32[:])
-                nc.scalar.activation(
-                    out=flat[:, t, :], in_=z_r[:], func=ACT.Relu, scale=gamma4[:, t : t + 1], bias=beta4[:, t : t + 1]
-                )
-            return flat
+        def relu_part(c, t):
+            z_r = psum.tile([P, CHUNK], F32, name="z_r", bufs=1)
+            for r in range(R_TILES):
+                nc.tensor.transpose(z_r[:, r * P : (r + 1) * P], z[c, r][:, t::4], ident_f32[:])
+            nc.scalar.activation(
+                out=flat[c][:, t, :], in_=z_r[:], func=ACT.Relu, scale=gamma4[:, t : t + 1], bias=beta4[:, t : t + 1]
+            )
 
         def larger(source, first, end):
             slots = slice(first, end)
@@ -282,7 +290,7 @@ def tile_kanlinear_pa_kernel(
             )
 
         def interleave(engine, source, first):
-            words = work.tile([P, 4 * CHUNK], BF16, name="words", align_bytes=64, bufs=4)
+            words = work.tile([P, 4 * CHUNK], BF16, name="words", align_bytes=64, bufs=3)
             engine.tensor_scalar(
                 out=words[:].rearrange("p (n t) -> p n t", t=4),
                 in0=source[:, first : first + 4, :].rearrange("p t n -> p n t"),
@@ -290,13 +298,13 @@ def tile_kanlinear_pa_kernel(
             )
             return words
 
-        def quantise(c, slot, source):
+        def quantise(c, slot, source, rows=slice(0, CHUNK)):
             nc.vector.quantize_mx(
-                out=codes[c][:, slot, :].bitcast(FP8X4), scales=planes[c][:, slot, :], in_=source[:]
+                out=codes[c][:, slot, rows].bitcast(FP8X4), scales=planes[c][:, slot, rows], in_=source[:]
             )
 
-        def multiply(c, slot, weights, plane, start, stop):
-            for r in range(R_TILES):
+        def multiply(c, slot, weights, plane, start, stop, tiles=range(R_TILES)):
+            for r in tiles:
                 n_cols = slice(r * P, (r + 1) * P)
                 nc.tensor.matmul_mx(
                     out=acc[c, r][:],
@@ -308,36 +316,35 @@ def tile_kanlinear_pa_kernel(
                     stop=stop,
                 )
 
-        def multiply_words(c, a, i):
+        def multiply_words(c, a, i, tiles=range(R_TILES)):
             for m in range(MASKS):
                 multiply(
                     c, 1 + WORDS * a + i, w_words[:, m, a, i, :], 1 + MASKS * a + m,
                     start=(a == 0 and i == 0 and m == 0),
                     stop=(a == GROUPS - 1 and i == WORDS - 1 and m == MASKS - 1),
+                    tiles=tiles,
                 )
 
-        def add_bias_and_store(c):
-            for r in range(R_TILES):
-                result = work.tile([P, UNITS], F32, name="result", bufs=3)
+        def add_bias_and_store(c, tiles):
+            for r in tiles:
+                result = work.tile([P, UNITS], F32, name="result", bufs=4)
                 nc.vector.tensor_add(out=result[:], in0=acc[c, r][:], in1=bias_bf[:])
                 row0 = (c * R_TILES + r) * P
                 nc.sync.dma_start(out=out[row0 : row0 + P, :], in_=result[:])
 
-        statistics(0)
-        inverse_std(0)
-        normalise(0)
         features_to_partitions(*STEPS[0])
         squares(*STEPS[0])
-        statistics(1)
-        inverse_std(1)
+        row_statistics(1, range(1, R_TILES))
+        mean_and_variance(1)
+        rough_rstd(1)
         words = {}
         flat = {}
         bases = {}
         for t, (c, a, e) in enumerate(STEPS):
             last = t == len(STEPS) - 1
             if a == 0 and e == 0:
-                codes[c] = work.tile([P, 1 + GROUPS * WORDS, CHUNK], U32, name="codes", align_bytes=64, bufs=2)
-                planes[c] = work.tile([P, 1 + GROUPS * WORDS, CHUNK], U8, name="planes", align_bytes=64, bufs=2)
+                codes[c] = work.tile([P, 1 + GROUPS * WORDS, CHUNK], U32, name="codes", align_bytes=64, bufs=1)
+                planes[c] = work.tile([P, 1 + GROUPS * WORDS, CHUNK], U8, name="planes", align_bytes=64, bufs=1)
             if not last:
                 features_to_partitions(*STEPS[t + 1])
             cubes(c, a, e, 0, 1)
@@ -347,20 +354,25 @@ def tile_kanlinear_pa_kernel(
                     larger(bases[pc, pa], 4, 12)
                     for i in (1, 2):
                         words[i] = interleave(nc.gpsimd, bases[pc, pa], 4 * i)
-                bases[c, a] = work.tile([P, 2 * BASES, CHUNK], BF16, name="bases", bufs=2)
+                bases[c, a] = work.tile([P, 2 * BASES, CHUNK], BF16, name="bases", bufs=1)
             else:
                 words[0] = interleave(nc.gpsimd, bases[c, a], 0)
                 if a == 1:
                     relu_words = interleave(nc.gpsimd, flat[c], 0)
             cubes(c, a, e, 1, KNOTS)
             if a == 0 and e == 1 and c > 0:
-                add_bias_and_store(c - 1)
-            if not last:
-                squares(*STEPS[t + 1])
-            if a == 0 and e == 1:
-                flat[c] = relu_branch(c)
-            if t == 1:
+                add_bias_and_store(c - 1, range(R_TILES))
+            if t == 0:
+                fine_rstd(1)
                 normalise(1)
+            if a == 0 and e == 1:
+                flat[c] = work.tile([P, 4, CHUNK], BF16, name="relu_flat")
+                for part in range(4):
+                    relu_part(c, part)
+                    squares(*STEPS[t + 1], 2 * part, 2 * part + 2)
+                squares(*STEPS[t + 1], 8, KNOTS)
+            elif not last:
+                squares(*STEPS[t + 1])
             if e == 0:
                 left_side(a, e, 0)
                 if t > 0:
@@ -384,18 +396,22 @@ def tile_kanlinear_pa_kernel(
                     quantise(c, 0, relu_words)
                 right_side(a, e, 0)
                 right_side(a, e, 1)
-                left_side(a, e, 2)
                 if last:
+                    left_side(a, e, 2)
                     larger(bases[c, a], 4, 8)
-                for j in (3, 4, 5):
+                for j in (3, 4, 5) if last else (2, 3, 4, 5):
                     left_side(a, e, j)
                 if last:
-                    words[1] = interleave(nc.vector, bases[c, a], 4)
+                    words[1] = work.tile([P, 4 * CHUNK], BF16, name="words", align_bytes=64, bufs=3)
+                    nc.scalar.copy(
+                        out=words[1][:].rearrange("p (n t) -> p n t", t=4),
+                        in_=bases[c, a][:, 4:8, :].rearrange("p t n -> p n t"),
+                    )
                 right_side(a, e, 2)
                 right_side(a, e, 3)
+                right_side(a, e, 4)
                 if last:
                     quantise(c, WORDS * a + 2, words[1])
-                right_side(a, e, 4)
                 right_side(a, e, 5)
                 if a == 0:
                     for r in range(R_TILES):
@@ -404,8 +420,19 @@ def tile_kanlinear_pa_kernel(
                 if a == 1:
                     multiply(c, 0, w_base[:], 0, start=False, stop=False)
         multiply_words(c, a, 1)
-        larger(bases[c, a], 8, 12)
-        words[2] = interleave(nc.vector, bases[c, a], 8)
-        quantise(c, WORDS * a + 3, words[2])
-        multiply_words(c, a, 2)
-        add_bias_and_store(c)
+        half = CHUNK // 2
+        four = slice(8, 12)
+        half_words = {}
+        for h in range(2):
+            rows = slice(h * half, (h + 1) * half)
+            half_words[h] = work.tile([P, 4 * half], BF16, name="half_words%d" % h, align_bytes=64)
+            nc.vector.tensor_tensor(
+                out=half_words[h][:].rearrange("p (n t) -> p n t", t=4),
+                in0=left[:, four, rows].rearrange("p t n -> p n t"),
+                in1=right[:, four, rows].rearrange("p t n -> p n t"),
+                op=ALU.max,
+            )
+            quantise(c, WORDS * a + 3, half_words[h], rows)
+        for r in range(R_TILES):
+            multiply_words(c, a, 2, [r])
+        add_bias_and_store(c, range(R_TILES))

@@ -19,6 +19,7 @@ KNOTS = 10
 LN_EPS = 0.001
 GROUPS = 2
 TILES = 2 * GROUPS
+K_PASS = 512
 WORDS = 3
 TRUNCATED = 7
 MASKS = 3
@@ -163,9 +164,8 @@ def tile_kanlinear_pa_kernel(
             count = KNOTS - span
             gap[span] = const.tile([P, TILES, count], F32, name="gap%d" % span)
             g.tensor_sub(out=gap[span][:], in0=knot[:, :, span:KNOTS], in1=knot[:, :, 0:count])
-            if span < 4:
-                inv[span] = const.tile([P, TILES, count], F32, name="inv%d" % span)
-                nc.vector.reciprocal(out=inv[span][:], in_=gap[span][:])
+            inv[span] = const.tile([P, TILES, count], F32, name="inv%d" % span)
+            nc.vector.reciprocal(out=inv[span][:], in_=gap[span][:])
         rise = const.tile([P, TILES, TRUNCATED], F32)
         g.tensor_mul(out=rise[:], in0=inv[1][:, :, 0:7], in1=inv[2][:, :, 0:7])
         g.tensor_mul(out=rise[:], in0=rise[:], in1=inv[3][:, :, 0:7])
@@ -175,12 +175,14 @@ def tile_kanlinear_pa_kernel(
         g.tensor_mul(out=fall[:], in0=fall[:], in1=inv[3][:, :, 0:7])
         g.tensor_scalar(out=fall[:], in0=fall[:], scalar1=-1.0, scalar2=0.0, op0=ALU.mult, op1=ALU.add)
         g.tensor_mul(out=fall[:], in0=fall[:], in1=gamma_safe[:].unsqueeze(2).to_broadcast([P, TILES, TRUNCATED]))
-        neg_gap4 = const.tile([P, TILES, BASES], F32)
-        g.tensor_scalar(out=neg_gap4[:], in0=gap[4][:], scalar1=-1.0, scalar2=0.0, op0=ALU.mult, op1=ALU.add)
         c_low = const.tile([P, TILES, BASES], F32)
-        g.tensor_mul(out=c_low[:], in0=neg_gap4[:], in1=inv[1][:, :, 0:6])
+        g.tensor_mul(out=c_low[:], in0=gap[4][:], in1=inv[1][:, :, 0:6])
+        g.tensor_mul(out=rise[:, :, 6:7], in0=rise[:, :, 6:7], in1=c_low[:, :, 5:6])
+        g.tensor_scalar(out=c_low[:], in0=c_low[:], scalar1=-1.0, scalar2=0.0, op0=ALU.mult, op1=ALU.add)
         c_high = const.tile([P, TILES, BASES], F32)
-        g.tensor_mul(out=c_high[:], in0=neg_gap4[:], in1=inv[1][:, :, 3:9])
+        g.tensor_mul(out=c_high[:], in0=gap[4][:], in1=inv[1][:, :, 3:9])
+        g.tensor_mul(out=fall[:, :, 0:6], in0=fall[:, :, 0:6], in1=c_high[:])
+        g.tensor_mul(out=c_high[:, :, 0:5], in0=gap[1][:, :, 4:9], in1=inv[4][:, :, 1:6])
         gamma4 = const.tile([P, 4], F32)
         g.tensor_copy(out=gamma4[:], in_=gamma4_bf[:])
         beta4 = const.tile([P, 4], F32)
@@ -248,9 +250,9 @@ def tile_kanlinear_pa_kernel(
                     scale=gamma[:, q : q + 1], bias=offset[:, q, i : i + 1],
                 )
 
-        def cubes(c, a, e, first, end):
+        def cubes(c, a, e):
             q = 2 * a + e
-            for i in range(first, end):
+            for i in range(KNOTS):
                 cube = work.tile([P, CHUNK], F32, name="cube", bufs=8)
                 nc.vector.scalar_tensor_tensor(
                     out=cube[:], in0=z_v[c, a, e][:], scalar=root[:, q, i : i + 1], in1=square[i][:],
@@ -271,9 +273,13 @@ def tile_kanlinear_pa_kernel(
 
         def right_side(a, e, j):
             nc.vector.scalar_tensor_tensor(
-                out=right[:, BASES * e + j, :], in0=neg[j + 3][:], scalar=c_high[:, 2 * a + e, j : j + 1],
-                in1=neg[j + 4][:], op0=ALU.mult, op1=ALU.add,
+                out=right[:, BASES * e + j, :], in0=neg[j + 4][:], scalar=c_high[:, 2 * a + e, j : j + 1],
+                in1=neg[j + 3][:], op0=ALU.mult, op1=ALU.subtract,
             )
+
+        def last_sides(engine, e):
+            engine.tensor_sub(out=left[:, BASES * e + 5, :], in0=pos[5][:], in1=pos[6][:])
+            engine.tensor_sub(out=right[:, BASES * e + 5, :], in0=neg[9][:], in1=neg[8][:])
 
         def relu_part(c, t):
             z_r = psum.tile([P, CHUNK], F32, name="z_r", bufs=1)
@@ -297,6 +303,21 @@ def tile_kanlinear_pa_kernel(
                 scalar1=1.0, scalar2=0.0, op0=ALU.mult, op1=ALU.add,
             )
             return words
+
+        def interleave_on_scalar(source, first):
+            words = work.tile([P, 4 * CHUNK], BF16, name="words", align_bytes=64, bufs=3)
+            nc.scalar.copy(
+                out=words[:].rearrange("p (n t) -> p n t", t=4),
+                in_=source[:, first : first + 4, :].rearrange("p t n -> p n t"),
+            )
+            return words
+
+        def interleave_relu_on_scalar(c, h):
+            rows = slice(h * CHUNK // 2, (h + 1) * CHUNK // 2)
+            nc.scalar.copy(
+                out=relu_words[c][:].rearrange("p (n t) -> p n t", t=4)[:, rows, :],
+                in_=flat[c][:, :, rows].rearrange("p t n -> p n t"),
+            )
 
         def quantise(c, slot, source, rows=slice(0, CHUNK)):
             nc.vector.quantize_mx(
@@ -339,6 +360,7 @@ def tile_kanlinear_pa_kernel(
         rough_rstd(1)
         words = {}
         flat = {}
+        relu_words = {}
         bases = {}
         for t, (c, a, e) in enumerate(STEPS):
             last = t == len(STEPS) - 1
@@ -347,24 +369,21 @@ def tile_kanlinear_pa_kernel(
                 planes[c] = work.tile([P, 1 + GROUPS * WORDS, CHUNK], U8, name="planes", align_bytes=64, bufs=1)
             if not last:
                 features_to_partitions(*STEPS[t + 1])
-            cubes(c, a, e, 0, 1)
-            if e == 0:
-                if t > 0:
-                    pc, pa, pe = STEPS[t - 1]
-                    larger(bases[pc, pa], 4, 12)
-                    for i in (1, 2):
-                        words[i] = interleave(nc.gpsimd, bases[pc, pa], 4 * i)
-                bases[c, a] = work.tile([P, 2 * BASES, CHUNK], BF16, name="bases", bufs=1)
-            else:
+            if e == 0 and t > 0:
+                pc, pa, pe = STEPS[t - 1]
+                for i in (1, 2):
+                    words[i] = interleave(nc.gpsimd, bases[pc, pa], 4 * i)
+            elif e == 1:
                 words[0] = interleave(nc.gpsimd, bases[c, a], 0)
-                if a == 1:
-                    relu_words = interleave(nc.gpsimd, flat[c], 0)
-            cubes(c, a, e, 1, KNOTS)
+                last_sides(nc.gpsimd, 0)
+            cubes(c, a, e)
             if a == 0 and e == 1 and c > 0:
                 add_bias_and_store(c - 1, range(R_TILES))
             if t == 0:
                 fine_rstd(1)
                 normalise(1)
+            if e == 0:
+                bases[c, a] = work.tile([P, 2 * BASES, CHUNK], BF16, name="bases", bufs=1)
             if a == 0 and e == 1:
                 flat[c] = work.tile([P, 4, CHUNK], BF16, name="relu_flat")
                 for part in range(4):
@@ -375,44 +394,48 @@ def tile_kanlinear_pa_kernel(
                 squares(*STEPS[t + 1])
             if e == 0:
                 left_side(a, e, 0)
-                if t > 0:
-                    quantise(pc, WORDS * pa + 2, words[1])
                 left_side(a, e, 1)
                 if t > 0:
-                    quantise(pc, WORDS * pa + 3, words[2])
-                for j in (2, 3, 4, 5):
+                    quantise(pc, WORDS * pa + 2, words[1])
+                for j in (2, 3, 4):
                     left_side(a, e, j)
-                for j in range(BASES):
+                for j in range(3):
                     right_side(a, e, j)
+                for j in (3, 4):
+                    right_side(a, e, j)
+                if t > 0:
+                    quantise(pc, WORDS * pa + 3, words[2])
                 larger(bases[c, a], 0, 4)
                 if t > 0:
                     multiply_words(pc, pa, 1)
                     multiply_words(pc, pa, 2)
             else:
                 left_side(a, e, 0)
-                quantise(c, 1 + WORDS * a, words[0])
+                if last:
+                    quantise(c, 1 + WORDS * a, words[0])
                 left_side(a, e, 1)
-                if a == 1:
-                    quantise(c, 0, relu_words)
                 right_side(a, e, 0)
                 right_side(a, e, 1)
                 if last:
                     left_side(a, e, 2)
                     larger(bases[c, a], 4, 8)
-                for j in (3, 4, 5) if last else (2, 3, 4, 5):
+                    words[1] = interleave_on_scalar(bases[c, a], 4)
+                for j in (3, 4) if last else (2, 3, 4):
                     left_side(a, e, j)
+                if a == 1:
+                    relu_words[c] = interleave(nc.vector, flat[c], 0)
+                if a == 1:
+                    quantise(c, 0, relu_words[c])
+                for j in (2, 3, 4):
+                    right_side(a, e, j)
+                    if last and j == 3:
+                        quantise(c, WORDS * a + 2, words[1])
                 if last:
-                    words[1] = work.tile([P, 4 * CHUNK], BF16, name="words", align_bytes=64, bufs=3)
-                    nc.scalar.copy(
-                        out=words[1][:].rearrange("p (n t) -> p n t", t=4),
-                        in_=bases[c, a][:, 4:8, :].rearrange("p t n -> p n t"),
-                    )
-                right_side(a, e, 2)
-                right_side(a, e, 3)
-                right_side(a, e, 4)
-                if last:
-                    quantise(c, WORDS * a + 2, words[1])
-                right_side(a, e, 5)
+                    last_sides(nc.vector, e)
+                else:
+                    last_sides(nc.vector, e)
+                    quantise(c, 1 + WORDS * a, words[0])
+                    larger(bases[c, a], 4, 12)
                 if a == 0:
                     for r in range(R_TILES):
                         acc[c, r] = psum.tile([P, UNITS], F32, name="acc", bufs=R_TILES)
@@ -420,19 +443,19 @@ def tile_kanlinear_pa_kernel(
                 if a == 1:
                     multiply(c, 0, w_base[:], 0, start=False, stop=False)
         multiply_words(c, a, 1)
-        half = CHUNK // 2
         four = slice(8, 12)
-        half_words = {}
-        for h in range(2):
-            rows = slice(h * half, (h + 1) * half)
-            half_words[h] = work.tile([P, 4 * half], BF16, name="half_words%d" % h, align_bytes=64)
-            nc.vector.tensor_tensor(
-                out=half_words[h][:].rearrange("p (n t) -> p n t", t=4),
-                in0=left[:, four, rows].rearrange("p t n -> p n t"),
-                in1=right[:, four, rows].rearrange("p t n -> p n t"),
-                op=ALU.max,
-            )
-            quantise(c, WORDS * a + 3, half_words[h], rows)
-        for r in range(R_TILES):
-            multiply_words(c, a, 2, [r])
+        tile_words = {}
+        for r in range(R_TILES + 1):
+            if r < R_TILES:
+                rows = slice(r * P, (r + 1) * P)
+                tile_words[r] = work.tile([P, K_PASS], BF16, name="tile_words", align_bytes=64, bufs=2)
+                nc.vector.tensor_tensor(
+                    out=tile_words[r][:].rearrange("p (n t) -> p n t", t=4),
+                    in0=left[:, four, rows].rearrange("p t n -> p n t"),
+                    in1=right[:, four, rows].rearrange("p t n -> p n t"),
+                    op=ALU.max,
+                )
+            if r > 0:
+                quantise(c, WORDS * a + 3, tile_words[r - 1], slice((r - 1) * P, r * P))
+                multiply_words(c, a, 2, [r - 1])
         add_bias_and_store(c, range(R_TILES))

@@ -19,6 +19,7 @@ KNOTS = 10
 LN_EPS = 0.001
 GROUPS = 2
 TILES = 2 * GROUPS
+TENSOR_SUM = 2
 K_PASS = 512
 WORDS = 3
 TRUNCATED = 7
@@ -92,6 +93,7 @@ def tile_kanlinear_pa_kernel(
         mean_var = {}
         var_eps = {}
         rstd0 = {}
+        newton = {}
         rstd = {}
         z = {}
         for c in range(CHUNKS):
@@ -112,16 +114,19 @@ def tile_kanlinear_pa_kernel(
             rstd0[c] = work.tile([P, R_TILES], F32, name="rstd0", bufs=2)
             nc.scalar.activation(out=rstd0[c][:], in_=var_eps[c][:], func=ACT.Abs_reciprocal_sqrt)
 
-        def fine_rstd(c):
-            newton = work.tile([P, R_TILES], F32, name="newton", bufs=2)
-            nc.vector.scalar_tensor_tensor(
-                out=newton[:], in0=rstd0[c][:], scalar=-0.5, in1=rstd0[c][:], op0=ALU.mult, op1=ALU.mult
-            )
-            nc.vector.tensor_mul(out=newton[:], in0=newton[:], in1=var_eps[c][:])
-            rstd[c] = work.tile([P, R_TILES], F32, name="rstd", bufs=2)
-            nc.vector.scalar_tensor_tensor(
-                out=rstd[c][:], in0=newton[:], scalar=1.5, in1=rstd0[c][:], op0=ALU.add, op1=ALU.mult
-            )
+        def refine_rstd(c, part):
+            if part == 0:
+                newton[c] = work.tile([P, R_TILES], F32, name="newton", bufs=2)
+                nc.vector.scalar_tensor_tensor(
+                    out=newton[c][:], in0=rstd0[c][:], scalar=-0.5, in1=rstd0[c][:], op0=ALU.mult, op1=ALU.mult
+                )
+            elif part == 1:
+                nc.vector.tensor_mul(out=newton[c][:], in0=newton[c][:], in1=var_eps[c][:])
+            else:
+                rstd[c] = work.tile([P, R_TILES], F32, name="rstd", bufs=2)
+                nc.vector.scalar_tensor_tensor(
+                    out=rstd[c][:], in0=newton[c][:], scalar=1.5, in1=rstd0[c][:], op0=ALU.add, op1=ALU.mult
+                )
 
         def normalise(c):
             for r in range(R_TILES):
@@ -135,7 +140,8 @@ def tile_kanlinear_pa_kernel(
         mean_and_variance(0)
         rough_rstd(0)
         row_statistics(1, [0])
-        fine_rstd(0)
+        for part in range(3):
+            refine_rstd(0, part)
         normalise(0)
 
         g = nc.gpsimd
@@ -164,7 +170,9 @@ def tile_kanlinear_pa_kernel(
             count = KNOTS - span
             gap[span] = const.tile([P, TILES, count], F32, name="gap%d" % span)
             g.tensor_sub(out=gap[span][:], in0=knot[:, :, span:KNOTS], in1=knot[:, :, 0:count])
-            inv[span] = const.tile([P, TILES, count], F32, name="inv%d" % span)
+        row_statistics(1, range(1, R_TILES))
+        for span in (1, 2, 3, 4):
+            inv[span] = const.tile([P, TILES, KNOTS - span], F32, name="inv%d" % span)
             nc.vector.reciprocal(out=inv[span][:], in_=gap[span][:])
         rise = const.tile([P, TILES, TRUNCATED], F32)
         g.tensor_mul(out=rise[:], in0=inv[1][:, :, 0:7], in1=inv[2][:, :, 0:7])
@@ -183,6 +191,11 @@ def tile_kanlinear_pa_kernel(
         g.tensor_mul(out=c_high[:], in0=gap[4][:], in1=inv[1][:, :, 3:9])
         g.tensor_mul(out=fall[:, :, 0:6], in0=fall[:, :, 0:6], in1=c_high[:])
         g.tensor_mul(out=c_high[:, :, 0:5], in0=gap[1][:, :, 4:9], in1=inv[4][:, :, 1:6])
+        ratio_diag = const.tile([P, TILES, P], F32)
+        for q in range(TILES):
+            g.tensor_mul(
+                out=ratio_diag[:, q, :], in0=ident_f32[:], in1=c_low[:, q, TENSOR_SUM : TENSOR_SUM + 1].to_broadcast([P, P])
+            )
         gamma4 = const.tile([P, 4], F32)
         g.tensor_copy(out=gamma4[:], in_=gamma4_bf[:])
         beta4 = const.tile([P, 4], F32)
@@ -271,6 +284,13 @@ def tile_kanlinear_pa_kernel(
                 in1=pos[j][:], op0=ALU.mult, op1=ALU.add,
             )
 
+        def left_side_on_tensor(a, e):
+            j = TENSOR_SUM
+            total = psum.tile([P, CHUNK], F32, name="z_r", bufs=1)
+            nc.tensor.matmul(total[:], lhsT=ident_f32[:], rhs=pos[j][:], start=True, stop=False)
+            nc.tensor.matmul(total[:], lhsT=ratio_diag[:, 2 * a + e, :], rhs=pos[j + 1][:], start=False, stop=True)
+            return total
+
         def right_side(a, e, j):
             nc.vector.scalar_tensor_tensor(
                 out=right[:, BASES * e + j, :], in0=neg[j + 4][:], scalar=c_high[:, 2 * a + e, j : j + 1],
@@ -355,7 +375,6 @@ def tile_kanlinear_pa_kernel(
 
         features_to_partitions(*STEPS[0])
         squares(*STEPS[0])
-        row_statistics(1, range(1, R_TILES))
         mean_and_variance(1)
         rough_rstd(1)
         words = {}
@@ -379,12 +398,15 @@ def tile_kanlinear_pa_kernel(
             cubes(c, a, e)
             if a == 0 and e == 1 and c > 0:
                 add_bias_and_store(c - 1, range(R_TILES))
-            if t == 0:
-                fine_rstd(1)
-                normalise(1)
             if e == 0:
                 bases[c, a] = work.tile([P, 2 * BASES, CHUNK], BF16, name="bases", bufs=1)
-            if a == 0 and e == 1:
+            on_tensor = t in (1, 4, 6)
+            if on_tensor:
+                total = left_side_on_tensor(a, e)
+                squares(*STEPS[t + 1], 0, 3)
+                nc.scalar.copy(out=left[:, BASES * e + TENSOR_SUM, :], in_=total[:])
+                squares(*STEPS[t + 1], 3, KNOTS)
+            elif t in (3, 5):
                 flat[c] = work.tile([P, 4, CHUNK], BF16, name="relu_flat")
                 for part in range(4):
                     relu_part(c, part)
@@ -398,16 +420,26 @@ def tile_kanlinear_pa_kernel(
                 if t > 0:
                     quantise(pc, WORDS * pa + 2, words[1])
                 for j in (2, 3, 4):
-                    left_side(a, e, j)
-                for j in range(3):
+                    if t == 0:
+                        refine_rstd(1, j - 2)
+                    if j != 2 or not on_tensor:
+                        left_side(a, e, j)
+                for j in range(5):
                     right_side(a, e, j)
-                for j in (3, 4):
-                    right_side(a, e, j)
+                if t == 0:
+                    normalise(1)
+                if t == 4:
+                    relu_words[0] = interleave(nc.vector, flat[0], 0)
                 if t > 0:
                     quantise(pc, WORDS * pa + 3, words[2])
+                if t == 4:
+                    quantise(0, 0, relu_words[0])
                 larger(bases[c, a], 0, 4)
                 if t > 0:
                     multiply_words(pc, pa, 1)
+                if t == 4:
+                    multiply(0, 0, w_base[:], 0, start=False, stop=False)
+                if t > 0:
                     multiply_words(pc, pa, 2)
             else:
                 left_side(a, e, 0)
@@ -420,14 +452,14 @@ def tile_kanlinear_pa_kernel(
                     left_side(a, e, 2)
                     larger(bases[c, a], 4, 8)
                     words[1] = interleave_on_scalar(bases[c, a], 4)
-                for j in (3, 4) if last else (2, 3, 4):
+                for j in (3, 4) if last or on_tensor else (2, 3, 4):
                     left_side(a, e, j)
-                if a == 1:
+                if last:
                     relu_words[c] = interleave(nc.vector, flat[c], 0)
-                if a == 1:
-                    quantise(c, 0, relu_words[c])
                 for j in (2, 3, 4):
                     right_side(a, e, j)
+                    if last and j == 2:
+                        quantise(c, 0, relu_words[c])
                     if last and j == 3:
                         quantise(c, WORDS * a + 2, words[1])
                 if last:
@@ -440,7 +472,7 @@ def tile_kanlinear_pa_kernel(
                     for r in range(R_TILES):
                         acc[c, r] = psum.tile([P, UNITS], F32, name="acc", bufs=R_TILES)
                 multiply_words(c, a, 0)
-                if a == 1:
+                if last:
                     multiply(c, 0, w_base[:], 0, start=False, stop=False)
         multiply_words(c, a, 1)
         four = slice(8, 12)

@@ -19,7 +19,6 @@ KNOTS = 10
 LN_EPS = 0.001
 GROUPS = 2
 TILES = 2 * GROUPS
-TENSOR_SUM = 2
 K_PASS = 512
 WORDS = 3
 TRUNCATED = 7
@@ -191,11 +190,6 @@ def tile_kanlinear_pa_kernel(
         g.tensor_mul(out=c_high[:], in0=gap[4][:], in1=inv[1][:, :, 3:9])
         g.tensor_mul(out=fall[:, :, 0:6], in0=fall[:, :, 0:6], in1=c_high[:])
         g.tensor_mul(out=c_high[:, :, 0:5], in0=gap[1][:, :, 4:9], in1=inv[4][:, :, 1:6])
-        ratio_diag = const.tile([P, TILES, P], F32)
-        for q in range(TILES):
-            g.tensor_mul(
-                out=ratio_diag[:, q, :], in0=ident_f32[:], in1=c_low[:, q, TENSOR_SUM : TENSOR_SUM + 1].to_broadcast([P, P])
-            )
         gamma4 = const.tile([P, 4], F32)
         g.tensor_copy(out=gamma4[:], in_=gamma4_bf[:])
         beta4 = const.tile([P, 4], F32)
@@ -283,13 +277,6 @@ def tile_kanlinear_pa_kernel(
                 out=left[:, BASES * e + j, :], in0=pos[j + 1][:], scalar=c_low[:, 2 * a + e, j : j + 1],
                 in1=pos[j][:], op0=ALU.mult, op1=ALU.add,
             )
-
-        def left_side_on_tensor(a, e):
-            j = TENSOR_SUM
-            total = psum.tile([P, CHUNK], F32, name="z_r", bufs=1)
-            nc.tensor.matmul(total[:], lhsT=ident_f32[:], rhs=pos[j][:], start=True, stop=False)
-            nc.tensor.matmul(total[:], lhsT=ratio_diag[:, 2 * a + e, :], rhs=pos[j + 1][:], start=False, stop=True)
-            return total
 
         def right_side(a, e, j):
             nc.vector.scalar_tensor_tensor(
@@ -400,13 +387,7 @@ def tile_kanlinear_pa_kernel(
                 add_bias_and_store(c - 1, range(R_TILES))
             if e == 0:
                 bases[c, a] = work.tile([P, 2 * BASES, CHUNK], BF16, name="bases", bufs=1)
-            on_tensor = t in (1, 4, 6)
-            if on_tensor:
-                total = left_side_on_tensor(a, e)
-                squares(*STEPS[t + 1], 0, 3)
-                nc.scalar.copy(out=left[:, BASES * e + TENSOR_SUM, :], in_=total[:])
-                squares(*STEPS[t + 1], 3, KNOTS)
-            elif t in (3, 5):
+            if t in (3, 5):
                 flat[c] = work.tile([P, 4, CHUNK], BF16, name="relu_flat")
                 for part in range(4):
                     relu_part(c, part)
@@ -422,8 +403,7 @@ def tile_kanlinear_pa_kernel(
                 for j in (2, 3, 4):
                     if t == 0:
                         refine_rstd(1, j - 2)
-                    if j != 2 or not on_tensor:
-                        left_side(a, e, j)
+                    left_side(a, e, j)
                 for j in range(5):
                     right_side(a, e, j)
                 if t == 0:
@@ -452,7 +432,7 @@ def tile_kanlinear_pa_kernel(
                     left_side(a, e, 2)
                     larger(bases[c, a], 4, 8)
                     words[1] = interleave_on_scalar(bases[c, a], 4)
-                for j in (3, 4) if last or on_tensor else (2, 3, 4):
+                for j in (3, 4) if last else (2, 3, 4):
                     left_side(a, e, j)
                 if last:
                     relu_words[c] = interleave(nc.vector, flat[c], 0)

@@ -71,12 +71,12 @@ def tile_kanlinear_pa_kernel(
                 in_=grid[0].rearrange("(a p e) i -> p a (e i)", a=GROUPS, e=2),
             )
             nc.scalar.dma_start(
-                out=gamma_bf[:].rearrange("p (a e) -> p a e", e=2),
-                in_=ln_gamma.rearrange("(a p e) -> p a e", a=GROUPS, e=2),
-            )
-            nc.scalar.dma_start(
                 out=beta_bf[:].rearrange("p (a e) -> p a e", e=2),
                 in_=ln_beta.rearrange("(a p e) -> p a e", a=GROUPS, e=2),
+            )
+            nc.scalar.dma_start(
+                out=gamma_bf[:].rearrange("p (a e) -> p a e", e=2),
+                in_=ln_gamma.rearrange("(a p e) -> p a e", a=GROUPS, e=2),
             )
             nc.scalar.dma_start(out=gamma4_bf[:], in_=ln_gamma.rearrange("(p t) -> p t", t=4))
             nc.scalar.dma_start(out=beta4_bf[:], in_=ln_beta.rearrange("(p t) -> p t", t=4))
@@ -145,51 +145,48 @@ def tile_kanlinear_pa_kernel(
 
         g = nc.gpsimd
         gamma = const.tile([P, TILES], F32)
-        g.tensor_copy(out=gamma[:], in_=gamma_bf[:])
-        beta = const.tile([P, TILES], F32)
-        g.tensor_copy(out=beta[:], in_=beta_bf[:])
-        knot = const.tile([P, TILES, KNOTS], F32)
-        g.tensor_copy(out=knot[:], in_=knots_bf[:])
-        gamma_sq = const.tile([P, TILES], F32)
-        g.tensor_mul(out=gamma_sq[:], in0=gamma[:], in1=gamma[:])
-        gamma_safe = const.tile([P, TILES], F32)
-        g.tensor_scalar(out=gamma_safe[:], in0=gamma_sq[:], scalar1=1e-24, scalar2=1.0, op0=ALU.is_ge, op1=ALU.mult)
-        g.tensor_mul(out=gamma_safe[:], in0=gamma_safe[:], in1=gamma[:])
-        g.tensor_scalar(out=gamma_sq[:], in0=gamma_sq[:], scalar1=1e-24, scalar2=1e-12, op0=ALU.is_lt, op1=ALU.mult)
-        g.tensor_add(out=gamma_safe[:], in0=gamma_safe[:], in1=gamma_sq[:])
-        inv_gamma = const.tile([P, TILES], F32)
-        nc.vector.reciprocal(out=inv_gamma[:], in_=gamma_safe[:])
+        nc.scalar.copy(out=gamma[:], in_=gamma_bf[:])
         offset = const.tile([P, TILES, KNOTS], F32)
-        g.tensor_sub(out=offset[:], in0=beta[:].unsqueeze(2).to_broadcast([P, TILES, KNOTS]), in1=knot[:])
-        root = const.tile([P, TILES, KNOTS], F32)
-        g.tensor_mul(out=root[:], in0=offset[:], in1=inv_gamma[:].unsqueeze(2).to_broadcast([P, TILES, KNOTS]))
+        g.tensor_sub(out=offset[:], in0=beta_bf[:].unsqueeze(2).to_broadcast([P, TILES, KNOTS]), in1=knots_bf[:])
+        gamma_safe = const.tile([P, TILES], F32)
+        g.tensor_mul(out=gamma_safe[:], in0=gamma_bf[:], in1=gamma_bf[:])
         gap = {}
         inv = {}
         for span in (1, 2, 3, 4):
-            count = KNOTS - span
-            gap[span] = const.tile([P, TILES, count], F32, name="gap%d" % span)
-            g.tensor_sub(out=gap[span][:], in0=knot[:, :, span:KNOTS], in1=knot[:, :, 0:count])
+            gap[span] = const.tile([P, TILES, KNOTS - span], F32, name="gap%d" % span)
+            g.tensor_sub(out=gap[span][:], in0=knots_bf[:, :, span:KNOTS], in1=knots_bf[:, :, 0 : KNOTS - span])
+            if span == 1:
+                g.tensor_scalar(
+                    out=gamma_safe[:], in0=gamma_safe[:], scalar1=1e-24, scalar2=2e-12, op0=ALU.is_lt, op1=ALU.mult
+                )
+            if span == 2:
+                g.tensor_add(out=gamma_safe[:], in0=gamma_safe[:], in1=gamma_bf[:])
         row_statistics(1, range(1, R_TILES))
+        inv_gamma = const.tile([P, TILES], F32)
+        nc.vector.reciprocal(out=inv_gamma[:], in_=gamma_safe[:])
         for span in (1, 2, 3, 4):
             inv[span] = const.tile([P, TILES, KNOTS - span], F32, name="inv%d" % span)
             nc.vector.reciprocal(out=inv[span][:], in_=gap[span][:])
+        neg_gamma = const.tile([P, TILES], F32)
+        g.tensor_scalar(out=neg_gamma[:], in0=gamma_safe[:], scalar1=-1.0, scalar2=0.0, op0=ALU.mult, op1=ALU.add)
+        root = const.tile([P, TILES, KNOTS], F32)
+        g.tensor_mul(out=root[:], in0=offset[:], in1=inv_gamma[:].unsqueeze(2).to_broadcast([P, TILES, KNOTS]))
         rise = const.tile([P, TILES, TRUNCATED], F32)
         g.tensor_mul(out=rise[:], in0=inv[1][:, :, 0:7], in1=inv[2][:, :, 0:7])
-        g.tensor_mul(out=rise[:], in0=rise[:], in1=inv[3][:, :, 0:7])
-        g.tensor_mul(out=rise[:], in0=rise[:], in1=gamma_safe[:].unsqueeze(2).to_broadcast([P, TILES, TRUNCATED]))
         fall = const.tile([P, TILES, TRUNCATED], F32)
         g.tensor_mul(out=fall[:], in0=inv[1][:, :, 2:9], in1=inv[2][:, :, 1:8])
+        g.tensor_mul(out=rise[:], in0=rise[:], in1=inv[3][:, :, 0:7])
         g.tensor_mul(out=fall[:], in0=fall[:], in1=inv[3][:, :, 0:7])
-        g.tensor_scalar(out=fall[:], in0=fall[:], scalar1=-1.0, scalar2=0.0, op0=ALU.mult, op1=ALU.add)
-        g.tensor_mul(out=fall[:], in0=fall[:], in1=gamma_safe[:].unsqueeze(2).to_broadcast([P, TILES, TRUNCATED]))
-        c_low = const.tile([P, TILES, BASES], F32)
-        g.tensor_mul(out=c_low[:], in0=gap[4][:], in1=inv[1][:, :, 0:6])
-        g.tensor_mul(out=rise[:, :, 6:7], in0=rise[:, :, 6:7], in1=c_low[:, :, 5:6])
-        g.tensor_scalar(out=c_low[:], in0=c_low[:], scalar1=-1.0, scalar2=0.0, op0=ALU.mult, op1=ALU.add)
+        g.tensor_mul(out=rise[:], in0=rise[:], in1=gamma_safe[:].unsqueeze(2).to_broadcast([P, TILES, TRUNCATED]))
+        g.tensor_mul(out=fall[:], in0=fall[:], in1=neg_gamma[:].unsqueeze(2).to_broadcast([P, TILES, TRUNCATED]))
         c_high = const.tile([P, TILES, BASES], F32)
         g.tensor_mul(out=c_high[:], in0=gap[4][:], in1=inv[1][:, :, 3:9])
+        c_low = const.tile([P, TILES, BASES], F32)
+        g.tensor_mul(out=c_low[:], in0=gap[4][:], in1=inv[1][:, :, 0:6])
         g.tensor_mul(out=fall[:, :, 0:6], in0=fall[:, :, 0:6], in1=c_high[:])
+        g.tensor_mul(out=rise[:, :, 6:7], in0=rise[:, :, 6:7], in1=c_low[:, :, 5:6])
         g.tensor_mul(out=c_high[:, :, 0:5], in0=gap[1][:, :, 4:9], in1=inv[4][:, :, 1:6])
+        g.tensor_scalar(out=c_low[:], in0=c_low[:], scalar1=-1.0, scalar2=0.0, op0=ALU.mult, op1=ALU.add)
         gamma4 = const.tile([P, 4], F32)
         g.tensor_copy(out=gamma4[:], in_=gamma4_bf[:])
         beta4 = const.tile([P, 4], F32)

@@ -53,33 +53,29 @@ def tile_kanlinear_pa_kernel(
 
         x_bf = const.tile([P, ROWS // P, FEATURES], BF16)
         x_rows = x.rearrange("(r p) f -> p r f", p=P)
-        for r in range(R_TILES):
-            nc.sync.dma_start(out=x_bf[:, r, :], in_=x_rows[:, r, :])
-        for c in range(1, CHUNKS):
-            r_range = slice(c * R_TILES, (c + 1) * R_TILES)
-            nc.sync.dma_start(out=x_bf[:, r_range, :], in_=x_rows[:, r_range, :])
-
-        knots_bf = const.tile([P, TILES, KNOTS], BF16)
-        gamma_bf = const.tile([P, TILES], BF16)
-        beta_bf = const.tile([P, TILES], BF16)
+        knots_raw = const.tile([P, GROUPS, 32], BF16)
+        gamma_raw = const.tile([P, GROUPS, 16], BF16)
+        beta_raw = const.tile([P, GROUPS, 16], BF16)
         gamma4_bf = const.tile([P, 4], BF16)
         beta4_bf = const.tile([P, 4], BF16)
         bias_bf = const.tile([P, UNITS], BF16)
+        for r in range(R_TILES):
+            nc.sync.dma_start(out=x_bf[:, r, :], in_=x_rows[:, r, :])
         with nc.allow_non_contiguous_dma(reason="small per-feature tables"):
             nc.scalar.dma_start(
-                out=knots_bf[:].rearrange("p (a e) i -> p a (e i)", e=2),
-                in_=grid[0].rearrange("(a p e) i -> p a (e i)", a=GROUPS, e=2),
+                out=knots_raw[:, :, 0 : 2 * KNOTS], in_=grid[0].rearrange("(a p e) i -> p a (e i)", a=GROUPS, e=2)
             )
-            nc.scalar.dma_start(
-                out=beta_bf[:].rearrange("p (a e) -> p a e", e=2),
-                in_=ln_beta.rearrange("(a p e) -> p a e", a=GROUPS, e=2),
-            )
-            nc.scalar.dma_start(
-                out=gamma_bf[:].rearrange("p (a e) -> p a e", e=2),
-                in_=ln_gamma.rearrange("(a p e) -> p a e", a=GROUPS, e=2),
-            )
-            nc.scalar.dma_start(out=gamma4_bf[:], in_=ln_gamma.rearrange("(p t) -> p t", t=4))
-            nc.scalar.dma_start(out=beta4_bf[:], in_=ln_beta.rearrange("(p t) -> p t", t=4))
+            nc.sync.dma_start(out=beta_raw[:, :, 0:2], in_=ln_beta.rearrange("(a p e) -> p a e", a=GROUPS, e=2))
+            nc.scalar.dma_start(out=gamma_raw[:, :, 0:2], in_=ln_gamma.rearrange("(a p e) -> p a e", a=GROUPS, e=2))
+        for c in range(1, CHUNKS):
+            r_range = slice(c * R_TILES, (c + 1) * R_TILES)
+            nc.sync.dma_start(out=x_bf[:, r_range, :], in_=x_rows[:, r_range, :])
+        with nc.allow_non_contiguous_dma(reason="small per-feature tables"):
+            nc.sync.dma_start(out=gamma4_bf[:], in_=ln_gamma.rearrange("(p t) -> p t", t=4))
+            nc.sync.dma_start(out=beta4_bf[:], in_=ln_beta.rearrange("(p t) -> p t", t=4))
+        knots_in = knots_raw[:, :, 0 : 2 * KNOTS].rearrange("p a (e i) -> p a e i", e=2)
+        gamma_in = gamma_raw[:, :, 0:2]
+        beta_in = beta_raw[:, :, 0:2]
 
         w_base = const.tile([P, 4 * UNITS], U8, align_bytes=64)
         w_words = const.tile([P, MASKS, GROUPS, WORDS, 4 * UNITS], U8, align_bytes=64)
@@ -145,22 +141,29 @@ def tile_kanlinear_pa_kernel(
 
         g = nc.gpsimd
         gamma = const.tile([P, TILES], F32)
-        nc.scalar.copy(out=gamma[:], in_=gamma_bf[:])
+        nc.scalar.copy(out=gamma[:].rearrange("p (a e) -> p a e", e=2), in_=gamma_in)
         offset = const.tile([P, TILES, KNOTS], F32)
-        g.tensor_sub(out=offset[:], in0=beta_bf[:].unsqueeze(2).to_broadcast([P, TILES, KNOTS]), in1=knots_bf[:])
+        g.tensor_sub(
+            out=offset[:].rearrange("p (a e) i -> p a e i", e=2),
+            in0=beta_in.unsqueeze(3).to_broadcast([P, GROUPS, 2, KNOTS]), in1=knots_in,
+        )
         gamma_safe = const.tile([P, TILES], F32)
-        g.tensor_mul(out=gamma_safe[:], in0=gamma_bf[:], in1=gamma_bf[:])
+        gamma_pairs = gamma_safe[:].rearrange("p (a e) -> p a e", e=2)
+        g.tensor_mul(out=gamma_pairs, in0=gamma_in, in1=gamma_in)
         gap = {}
         inv = {}
         for span in (1, 2, 3, 4):
             gap[span] = const.tile([P, TILES, KNOTS - span], F32, name="gap%d" % span)
-            g.tensor_sub(out=gap[span][:], in0=knots_bf[:, :, span:KNOTS], in1=knots_bf[:, :, 0 : KNOTS - span])
+            g.tensor_sub(
+                out=gap[span][:].rearrange("p (a e) i -> p a e i", e=2),
+                in0=knots_in[:, :, :, span:KNOTS], in1=knots_in[:, :, :, 0 : KNOTS - span],
+            )
             if span == 1:
                 g.tensor_scalar(
                     out=gamma_safe[:], in0=gamma_safe[:], scalar1=1e-24, scalar2=2e-12, op0=ALU.is_lt, op1=ALU.mult
                 )
             if span == 2:
-                g.tensor_add(out=gamma_safe[:], in0=gamma_safe[:], in1=gamma_bf[:])
+                g.tensor_add(out=gamma_pairs, in0=gamma_pairs, in1=gamma_in)
         row_statistics(1, range(1, R_TILES))
         inv_gamma = const.tile([P, TILES], F32)
         nc.vector.reciprocal(out=inv_gamma[:], in_=gamma_safe[:])
@@ -193,7 +196,8 @@ def tile_kanlinear_pa_kernel(
         g.tensor_copy(out=beta4[:], in_=beta4_bf[:])
 
         for m in range(MASKS):
-            g.memset(w_words[:, m].rearrange("p a i c -> p (a i c)").bitcast(I32), 0)
+            for a in range(GROUPS):
+                g.memset(w_words[:, m, a].rearrange("p i c -> p (i c)").bitcast(I32), 0)
         nc.sync.dma_start(
             out=w_base[:].bitcast(I32),
             in_=base_weight_words[0].rearrange("p n t -> p (n t)").bitcast(I32),
@@ -238,7 +242,7 @@ def tile_kanlinear_pa_kernel(
 
         def features_to_partitions(c, a, e):
             z_s[c, a, e] = psum.tile([P, CHUNK], F32, name="z_s", bufs=1)
-            z_v[c, a, e] = psum.tile([P, CHUNK], F32, name="z_v", bufs=2)
+            z_v[c, a, e] = psum.tile([P, CHUNK], F32, name="z_v", bufs=1)
             for z_t in (z_s[c, a, e], z_v[c, a, e]):
                 for r in range(R_TILES):
                     nc.tensor.transpose(
@@ -286,7 +290,7 @@ def tile_kanlinear_pa_kernel(
             engine.tensor_sub(out=right[:, BASES * e + 5, :], in0=neg[9][:], in1=neg[8][:])
 
         def relu_part(c, t):
-            z_r = psum.tile([P, CHUNK], F32, name="z_r", bufs=1)
+            z_r = psum.tile([P, CHUNK], F32, name="z_r", bufs=2)
             for r in range(R_TILES):
                 nc.tensor.transpose(z_r[:, r * P : (r + 1) * P], z[c, r][:, t::4], ident_f32[:])
             nc.scalar.activation(
@@ -370,8 +374,6 @@ def tile_kanlinear_pa_kernel(
             if a == 0 and e == 0:
                 codes[c] = work.tile([P, 1 + GROUPS * WORDS, CHUNK], U32, name="codes", align_bytes=64, bufs=1)
                 planes[c] = work.tile([P, 1 + GROUPS * WORDS, CHUNK], U8, name="planes", align_bytes=64, bufs=1)
-            if not last:
-                features_to_partitions(*STEPS[t + 1])
             if e == 0 and t > 0:
                 pc, pa, pe = STEPS[t - 1]
                 for i in (1, 2):
@@ -380,6 +382,8 @@ def tile_kanlinear_pa_kernel(
                 words[0] = interleave(nc.gpsimd, bases[c, a], 0)
                 last_sides(nc.gpsimd, 0)
             cubes(c, a, e)
+            if not last:
+                features_to_partitions(*STEPS[t + 1])
             if a == 0 and e == 1 and c > 0:
                 add_bias_and_store(c - 1, range(R_TILES))
             if e == 0:
@@ -439,10 +443,8 @@ def tile_kanlinear_pa_kernel(
                         quantise(c, 0, relu_words[c])
                     if last and j == 3:
                         quantise(c, WORDS * a + 2, words[1])
-                if last:
-                    last_sides(nc.vector, e)
-                else:
-                    last_sides(nc.vector, e)
+                last_sides(nc.vector, e)
+                if not last:
                     quantise(c, 1 + WORDS * a, words[0])
                     larger(bases[c, a], 4, 12)
                 if a == 0:

from contextlib import ExitStack

import concourse.mybir as mybir
from concourse.masks import make_identity

F32 = mybir.dt.float32
BF16 = mybir.dt.bfloat16
I32 = mybir.dt.int32
U32 = mybir.dt.uint32
U8 = mybir.dt.uint8
FP8X4 = mybir.dt.float8_e4m3fn_x4
ALU = mybir.AluOpType
ACT = mybir.ActivationFunctionType

P = 128
ROWS, FEATURES, UNITS = 1024, 512, 512
BASES = 6
KNOTS = 10
LN_EPS = 0.001
GROUPS = 2
TILES = 2 * GROUPS
K_PASS = 512
WORDS = 3
TRUNCATED = 7
MASKS = 3
CHUNK = 512
R_TILES = CHUNK // P
CHUNKS = ROWS // CHUNK
STEPS = [(c, a, e) for c in range(CHUNKS) for a in range(GROUPS) for e in range(2)]

FLOPS = 2 * ROWS * (FEATURES + FEATURES * BASES) * UNITS


def tile_kanlinear_pa_kernel(
    tc,
    x,
    ln_gamma,
    ln_beta,
    base_weight_words,
    base_weight_scales,
    base_bias,
    spline_weight_words,
    spline_weight_scales,
    grid,
    out,
):
    nc = tc.nc
    with ExitStack() as stack:
        const = stack.enter_context(tc.tile_pool(name="const", bufs=1))
        work = stack.enter_context(tc.tile_pool(name="work", bufs=1))
        psum = stack.enter_context(tc.psum_pool(name="psum", bufs=2))
        stack.enter_context(tc.manual_schedule())

        x_bf = const.tile([P, ROWS // P, FEATURES], BF16)
        x_rows = x.rearrange("(r p) f -> p r f", p=P)
        knots_raw = const.tile([P, GROUPS, 32], BF16)
        gamma_raw = const.tile([P, GROUPS, 16], BF16)
        beta_raw = const.tile([P, GROUPS, 16], BF16)
        gamma4_bf = const.tile([P, 4], BF16)
        beta4_bf = const.tile([P, 4], BF16)
        bias_bf = const.tile([P, UNITS], BF16)
        for r in range(R_TILES):
            nc.sync.dma_start(out=x_bf[:, r, :], in_=x_rows[:, r, :])
        with nc.allow_non_contiguous_dma(reason="small per-feature tables"):
            nc.scalar.dma_start(
                out=knots_raw[:, :, 0 : 2 * KNOTS], in_=grid[0].rearrange("(a p e) i -> p a (e i)", a=GROUPS, e=2)
            )
            nc.sync.dma_start(out=beta_raw[:, :, 0:2], in_=ln_beta.rearrange("(a p e) -> p a e", a=GROUPS, e=2))
            nc.scalar.dma_start(out=gamma_raw[:, :, 0:2], in_=ln_gamma.rearrange("(a p e) -> p a e", a=GROUPS, e=2))
        for c in range(1, CHUNKS):
            r_range = slice(c * R_TILES, (c + 1) * R_TILES)
            nc.sync.dma_start(out=x_bf[:, r_range, :], in_=x_rows[:, r_range, :])
        with nc.allow_non_contiguous_dma(reason="small per-feature tables"):
            nc.sync.dma_start(out=gamma4_bf[:], in_=ln_gamma.rearrange("(p t) -> p t", t=4))
            nc.sync.dma_start(out=beta4_bf[:], in_=ln_beta.rearrange("(p t) -> p t", t=4))
        knots_in = knots_raw[:, :, 0 : 2 * KNOTS].rearrange("p a (e i) -> p a e i", e=2)
        gamma_in = gamma_raw[:, :, 0:2]
        beta_in = beta_raw[:, :, 0:2]

        w_base = const.tile([P, 4 * UNITS], U8, align_bytes=64)
        w_words = const.tile([P, MASKS, GROUPS, WORDS, 4 * UNITS], U8, align_bytes=64)
        w_planes = const.tile([P, 1 + GROUPS * MASKS, UNITS], U8, align_bytes=64)
        nc.vector.memset(w_planes[:].bitcast(I32), 0)
        ident_f32 = const.tile([P, P], F32)
        make_identity(nc, ident_f32[:])

        stats = {}
        mean_var = {}
        var_eps = {}
        rstd0 = {}
        newton = {}
        rstd = {}
        z = {}
        for c in range(CHUNKS):
            stats[c] = const.tile([P, R_TILES, 6], F32, name="stats%d" % c)
            mean_var[c] = const.tile([P, R_TILES, 2], F32, name="mean_var%d" % c)
            var_eps[c] = const.tile([P, R_TILES], F32, name="var_eps%d" % c)

        def row_statistics(c, tiles):
            for r in tiles:
                nc.vector.bn_stats(out=stats[c][:, r, :], in_=x_bf[:, c * R_TILES + r, :])

        def mean_and_variance(c):
            for r in range(R_TILES):
                nc.vector.bn_aggr(out=mean_var[c][:, r, :], in_=stats[c][:, r, :])
            nc.vector.tensor_scalar_add(out=var_eps[c][:], in0=mean_var[c][:, :, 1], scalar1=LN_EPS)

        def rough_rstd(c):
            rstd0[c] = work.tile([P, R_TILES], F32, name="rstd0", bufs=2)
            nc.scalar.activation(out=rstd0[c][:], in_=var_eps[c][:], func=ACT.Abs_reciprocal_sqrt)

        def refine_rstd(c, part):
            if part == 0:
                newton[c] = work.tile([P, R_TILES], F32, name="newton", bufs=2)
                nc.vector.scalar_tensor_tensor(
                    out=newton[c][:], in0=rstd0[c][:], scalar=-0.5, in1=rstd0[c][:], op0=ALU.mult, op1=ALU.mult
                )
            elif part == 1:
                nc.vector.tensor_mul(out=newton[c][:], in0=newton[c][:], in1=var_eps[c][:])
            else:
                rstd[c] = work.tile([P, R_TILES], F32, name="rstd", bufs=2)
                nc.vector.scalar_tensor_tensor(
                    out=rstd[c][:], in0=newton[c][:], scalar=1.5, in1=rstd0[c][:], op0=ALU.add, op1=ALU.mult
                )

        def normalise(c):
            for r in range(R_TILES):
                z[c, r] = work.tile([P, FEATURES], F32, name="z", bufs=ROWS // P)
                nc.vector.tensor_scalar(
                    out=z[c, r][:], in0=x_bf[:, c * R_TILES + r, :], scalar1=mean_var[c][:, r, 0:1],
                    scalar2=rstd[c][:, r : r + 1], op0=ALU.subtract, op1=ALU.mult,
                )

        row_statistics(0, range(R_TILES))
        mean_and_variance(0)
        rough_rstd(0)
        row_statistics(1, [0])
        for part in range(3):
            refine_rstd(0, part)
        normalise(0)

        g = nc.gpsimd
        gamma = const.tile([P, TILES], F32)
        nc.scalar.copy(out=gamma[:].rearrange("p (a e) -> p a e", e=2), in_=gamma_in)
        offset = const.tile([P, TILES, KNOTS], F32)
        g.tensor_sub(
            out=offset[:].rearrange("p (a e) i -> p a e i", e=2),
            in0=beta_in.unsqueeze(3).to_broadcast([P, GROUPS, 2, KNOTS]), in1=knots_in,
        )
        gamma_safe = const.tile([P, TILES], F32)
        gamma_pairs = gamma_safe[:].rearrange("p (a e) -> p a e", e=2)
        g.tensor_mul(out=gamma_pairs, in0=gamma_in, in1=gamma_in)
        gap = {}
        inv = {}
        for span in (1, 2, 3, 4):
            gap[span] = const.tile([P, TILES, KNOTS - span], F32, name="gap%d" % span)
            g.tensor_sub(
                out=gap[span][:].rearrange("p (a e) i -> p a e i", e=2),
                in0=knots_in[:, :, :, span:KNOTS], in1=knots_in[:, :, :, 0 : KNOTS - span],
            )
            if span == 1:
                g.tensor_scalar(
                    out=gamma_safe[:], in0=gamma_safe[:], scalar1=1e-24, scalar2=2e-12, op0=ALU.is_lt, op1=ALU.mult
                )
            if span == 2:
                g.tensor_add(out=gamma_pairs, in0=gamma_pairs, in1=gamma_in)
        row_statistics(1, range(1, R_TILES))
        inv_gamma = const.tile([P, TILES], F32)
        nc.vector.reciprocal(out=inv_gamma[:], in_=gamma_safe[:])
        for span in (1, 2, 3, 4):
            inv[span] = const.tile([P, TILES, KNOTS - span], F32, name="inv%d" % span)
            nc.vector.reciprocal(out=inv[span][:], in_=gap[span][:])
        neg_gamma = const.tile([P, TILES], F32)
        g.tensor_scalar(out=neg_gamma[:], in0=gamma_safe[:], scalar1=-1.0, scalar2=0.0, op0=ALU.mult, op1=ALU.add)
        root = const.tile([P, TILES, KNOTS], F32)
        g.tensor_mul(out=root[:], in0=offset[:], in1=inv_gamma[:].unsqueeze(2).to_broadcast([P, TILES, KNOTS]))
        rise = const.tile([P, TILES, TRUNCATED], F32)
        g.tensor_mul(out=rise[:], in0=inv[1][:, :, 0:7], in1=inv[2][:, :, 0:7])
        fall = const.tile([P, TILES, TRUNCATED], F32)
        g.tensor_mul(out=fall[:], in0=inv[1][:, :, 2:9], in1=inv[2][:, :, 1:8])
        g.tensor_mul(out=rise[:], in0=rise[:], in1=inv[3][:, :, 0:7])
        g.tensor_mul(out=fall[:], in0=fall[:], in1=inv[3][:, :, 0:7])
        g.tensor_mul(out=rise[:], in0=rise[:], in1=gamma_safe[:].unsqueeze(2).to_broadcast([P, TILES, TRUNCATED]))
        g.tensor_mul(out=fall[:], in0=fall[:], in1=neg_gamma[:].unsqueeze(2).to_broadcast([P, TILES, TRUNCATED]))
        c_high = const.tile([P, TILES, BASES], F32)
        g.tensor_mul(out=c_high[:], in0=gap[4][:], in1=inv[1][:, :, 3:9])
        c_low = const.tile([P, TILES, BASES], F32)
        g.tensor_mul(out=c_low[:], in0=gap[4][:], in1=inv[1][:, :, 0:6])
        g.tensor_mul(out=fall[:, :, 0:6], in0=fall[:, :, 0:6], in1=c_high[:])
        g.tensor_mul(out=rise[:, :, 6:7], in0=rise[:, :, 6:7], in1=c_low[:, :, 5:6])
        g.tensor_mul(out=c_high[:, :, 0:5], in0=gap[1][:, :, 4:9], in1=inv[4][:, :, 1:6])
        g.tensor_scalar(out=c_low[:], in0=c_low[:], scalar1=-1.0, scalar2=0.0, op0=ALU.mult, op1=ALU.add)
        gamma4 = const.tile([P, 4], F32)
        g.tensor_copy(out=gamma4[:], in_=gamma4_bf[:])
        beta4 = const.tile([P, 4], F32)
        g.tensor_copy(out=beta4[:], in_=beta4_bf[:])

        for m in range(MASKS):
            for a in range(GROUPS):
                g.memset(w_words[:, m, a].rearrange("p i c -> p (i c)").bitcast(I32), 0)
        nc.sync.dma_start(
            out=w_base[:].bitcast(I32),
            in_=base_weight_words[0].rearrange("p n t -> p (n t)").bitcast(I32),
        )
        scale_rows = spline_weight_scales.rearrange("g r n -> (g r) n").bitcast(I32).rearrange(
            "(a q i m) n -> q i a (m n)", a=GROUPS, q=4, i=4
        )
        for quadrant in range(4):
            live = slice(32 * quadrant, 32 * quadrant + 4)
            nc.sync.dma_start(
                out=w_planes[live, 0, :].bitcast(I32),
                in_=base_weight_scales[0, 4 * quadrant : 4 * quadrant + 4, :].bitcast(I32),
            )
            nc.sync.dma_start(
                out=w_planes[live, 1:, :].rearrange("i (a m) n -> i a (m n)", a=GROUPS).bitcast(I32),
                in_=scale_rows[quadrant],
            )
        word_rows = spline_weight_words.rearrange("g p n t -> (g p) (n t)").bitcast(I32).rearrange(
            "(a b u i) c -> u b a i c", a=GROUPS, u=8, i=WORDS
        )
        for m in range(MASKS):
            for u in range(8):
                words = [i for i in range(WORDS) if (3 * u + i) // 8 == m]
                if words:
                    run = slice(words[0], words[-1] + 1)
                    nc.sync.dma_start(
                        out=w_words[u:P:8, m, :, run, :].rearrange("b a i c -> b a (i c)").bitcast(I32),
                        in_=word_rows[u][:, :, run, :].rearrange("b a i c -> b a (i c)"),
                    )
        nc.sync.dma_start(out=bias_bf[:], in_=base_bias.partition_broadcast(P))

        z_s = {}
        z_v = {}
        square = {}
        codes = {}
        planes = {}
        acc = {}
        pos = {}
        neg = {}
        left = const.tile([P, 2 * BASES, CHUNK], BF16)
        right = const.tile([P, 2 * BASES, CHUNK], BF16)

        def features_to_partitions(c, a, e):
            z_s[c, a, e] = psum.tile([P, CHUNK], F32, name="z_s", bufs=1)
            z_v[c, a, e] = psum.tile([P, CHUNK], F32, name="z_v", bufs=1)
            for z_t in (z_s[c, a, e], z_v[c, a, e]):
                for r in range(R_TILES):
                    nc.tensor.transpose(
                        z_t[:, r * P : (r + 1) * P], z[c, r][:, 256 * a + e : 256 * (a + 1) : 2], ident_f32[:]
                    )

        def squares(c, a, e, first=0, end=KNOTS):
            q = 2 * a + e
            for i in range(first, end):
                square[i] = work.tile([P, CHUNK], F32, name="square%d" % i)
                nc.scalar.activation(
                    out=square[i][:], in_=z_s[c, a, e][:], func=ACT.Square,
                    scale=gamma[:, q : q + 1], bias=offset[:, q, i : i + 1],
                )

        def cubes(c, a, e):
            q = 2 * a + e
            for i in range(KNOTS):
                cube = work.tile([P, CHUNK], F32, name="cube", bufs=8)
                nc.vector.scalar_tensor_tensor(
                    out=cube[:], in0=z_v[c, a, e][:], scalar=root[:, q, i : i + 1], in1=square[i][:],
                    op0=ALU.add, op1=ALU.mult,
                )
                if i < TRUNCATED:
                    pos[i] = work.tile([P, CHUNK], F32, name="pos%d" % i)
                    nc.scalar.activation(out=pos[i][:], in_=cube[:], func=ACT.Relu, scale=rise[:, q, i : i + 1])
                if i >= 3:
                    neg[i] = work.tile([P, CHUNK], F32, name="neg%d" % i)
                    nc.scalar.activation(out=neg[i][:], in_=cube[:], func=ACT.Relu, scale=fall[:, q, i - 3 : i - 2])

        def left_side(a, e, j):
            nc.vector.scalar_tensor_tensor(
                out=left[:, BASES * e + j, :], in0=pos[j + 1][:], scalar=c_low[:, 2 * a + e, j : j + 1],
                in1=pos[j][:], op0=ALU.mult, op1=ALU.add,
            )

        def right_side(a, e, j):
            nc.vector.scalar_tensor_tensor(
                out=right[:, BASES * e + j, :], in0=neg[j + 4][:], scalar=c_high[:, 2 * a + e, j : j + 1],
                in1=neg[j + 3][:], op0=ALU.mult, op1=ALU.subtract,
            )

        def last_sides(engine, e):
            engine.tensor_sub(out=left[:, BASES * e + 5, :], in0=pos[5][:], in1=pos[6][:])
            engine.tensor_sub(out=right[:, BASES * e + 5, :], in0=neg[9][:], in1=neg[8][:])

        def relu_part(c, t):
            z_r = psum.tile([P, CHUNK], F32, name="z_r", bufs=2)
            for r in range(R_TILES):
                nc.tensor.transpose(z_r[:, r * P : (r + 1) * P], z[c, r][:, t::4], ident_f32[:])
            nc.scalar.activation(
                out=flat[c][:, t, :], in_=z_r[:], func=ACT.Relu, scale=gamma4[:, t : t + 1], bias=beta4[:, t : t + 1]
            )

        def larger(source, first, end):
            slots = slice(first, end)
            nc.vector.tensor_tensor(
                out=source[:, slots, :], in0=left[:, slots, :], in1=right[:, slots, :], op=ALU.max
            )

        def interleave(engine, source, first):
            words = work.tile([P, 4 * CHUNK], BF16, name="words", align_bytes=64, bufs=3)
            engine.tensor_scalar(
                out=words[:].rearrange("p (n t) -> p n t", t=4),
                in0=source[:, first : first + 4, :].rearrange("p t n -> p n t"),
                scalar1=1.0, scalar2=0.0, op0=ALU.mult, op1=ALU.add,
            )
            return words

        def interleave_on_scalar(source, first):
            words = work.tile([P, 4 * CHUNK], BF16, name="words", align_bytes=64, bufs=3)
            nc.scalar.copy(
                out=words[:].rearrange("p (n t) -> p n t", t=4),
                in_=source[:, first : first + 4, :].rearrange("p t n -> p n t"),
            )
            return words

        def interleave_relu_on_scalar(c, h):
            rows = slice(h * CHUNK // 2, (h + 1) * CHUNK // 2)
            nc.scalar.copy(
                out=relu_words[c][:].rearrange("p (n t) -> p n t", t=4)[:, rows, :],
                in_=flat[c][:, :, rows].rearrange("p t n -> p n t"),
            )

        def quantise(c, slot, source, rows=slice(0, CHUNK)):
            nc.vector.quantize_mx(
                out=codes[c][:, slot, rows].bitcast(FP8X4), scales=planes[c][:, slot, rows], in_=source[:]
            )

        def multiply(c, slot, weights, plane, start, stop, tiles=range(R_TILES)):
            for r in tiles:
                n_cols = slice(r * P, (r + 1) * P)
                nc.tensor.matmul_mx(
                    out=acc[c, r][:],
                    lhsT=codes[c][:, slot, n_cols].bitcast(FP8X4),
                    lhsT_scale=planes[c][:, slot, n_cols],
                    rhs=weights.bitcast(FP8X4),
                    rhs_scale=w_planes[:, plane, :],
                    start=start,
                    stop=stop,
                )

        def multiply_words(c, a, i, tiles=range(R_TILES)):
            for m in range(MASKS):
                multiply(
                    c, 1 + WORDS * a + i, w_words[:, m, a, i, :], 1 + MASKS * a + m,
                    start=(a == 0 and i == 0 and m == 0),
                    stop=(a == GROUPS - 1 and i == WORDS - 1 and m == MASKS - 1),
                    tiles=tiles,
                )

        def add_bias_and_store(c, tiles):
            for r in tiles:
                result = work.tile([P, UNITS], F32, name="result", bufs=4)
                nc.vector.tensor_add(out=result[:], in0=acc[c, r][:], in1=bias_bf[:])
                row0 = (c * R_TILES + r) * P
                nc.sync.dma_start(out=out[row0 : row0 + P, :], in_=result[:])

        features_to_partitions(*STEPS[0])
        squares(*STEPS[0])
        mean_and_variance(1)
        rough_rstd(1)
        words = {}
        flat = {}
        relu_words = {}
        bases = {}
        for t, (c, a, e) in enumerate(STEPS):
            last = t == len(STEPS) - 1
            if a == 0 and e == 0:
                codes[c] = work.tile([P, 1 + GROUPS * WORDS, CHUNK], U32, name="codes", align_bytes=64, bufs=1)
                planes[c] = work.tile([P, 1 + GROUPS * WORDS, CHUNK], U8, name="planes", align_bytes=64, bufs=1)
            if e == 0 and t > 0:
                pc, pa, pe = STEPS[t - 1]
                for i in (1, 2):
                    words[i] = interleave(nc.gpsimd, bases[pc, pa], 4 * i)
            elif e == 1:
                words[0] = interleave(nc.gpsimd, bases[c, a], 0)
                last_sides(nc.gpsimd, 0)
            cubes(c, a, e)
            if not last:
                features_to_partitions(*STEPS[t + 1])
            if a == 0 and e == 1 and c > 0:
                add_bias_and_store(c - 1, range(R_TILES))
            if e == 0:
                bases[c, a] = work.tile([P, 2 * BASES, CHUNK], BF16, name="bases", bufs=1)
            if t in (3, 5):
                flat[c] = work.tile([P, 4, CHUNK], BF16, name="relu_flat")
                for part in range(4):
                    relu_part(c, part)
                    squares(*STEPS[t + 1], 2 * part, 2 * part + 2)
                squares(*STEPS[t + 1], 8, KNOTS)
            elif not last:
                squares(*STEPS[t + 1])
            if e == 0:
                left_side(a, e, 0)
                left_side(a, e, 1)
                if t > 0:
                    quantise(pc, WORDS * pa + 2, words[1])
                for j in (2, 3, 4):
                    if t == 0:
                        refine_rstd(1, j - 2)
                    left_side(a, e, j)
                for j in range(5):
                    right_side(a, e, j)
                if t == 0:
                    normalise(1)
                if t == 4:
                    relu_words[0] = interleave(nc.vector, flat[0], 0)
                if t > 0:
                    quantise(pc, WORDS * pa + 3, words[2])
                if t == 4:
                    quantise(0, 0, relu_words[0])
                larger(bases[c, a], 0, 4)
                if t > 0:
                    multiply_words(pc, pa, 1)
                if t == 4:
                    multiply(0, 0, w_base[:], 0, start=False, stop=False)
                if t > 0:
                    multiply_words(pc, pa, 2)
            else:
                left_side(a, e, 0)
                if last:
                    quantise(c, 1 + WORDS * a, words[0])
                left_side(a, e, 1)
                right_side(a, e, 0)
                right_side(a, e, 1)
                if last:
                    left_side(a, e, 2)
                    larger(bases[c, a], 4, 8)
                    words[1] = interleave_on_scalar(bases[c, a], 4)
                for j in (3, 4) if last else (2, 3, 4):
                    left_side(a, e, j)
                if last:
                    relu_words[c] = interleave(nc.vector, flat[c], 0)
                for j in (2, 3, 4):
                    right_side(a, e, j)
                    if last and j == 2:
                        quantise(c, 0, relu_words[c])
                    if last and j == 3:
                        quantise(c, WORDS * a + 2, words[1])
                last_sides(nc.vector, e)
                if not last:
                    quantise(c, 1 + WORDS * a, words[0])
                    larger(bases[c, a], 4, 12)
                if a == 0:
                    for r in range(R_TILES):
                        acc[c, r] = psum.tile([P, UNITS], F32, name="acc", bufs=R_TILES)
                multiply_words(c, a, 0)
                if last:
                    multiply(c, 0, w_base[:], 0, start=False, stop=False)
        multiply_words(c, a, 1)
        four = slice(8, 12)
        tile_words = {}
        for r in range(R_TILES + 1):
            if r < R_TILES:
                rows = slice(r * P, (r + 1) * P)
                tile_words[r] = work.tile([P, K_PASS], BF16, name="tile_words", align_bytes=64, bufs=2)
                nc.vector.tensor_tensor(
                    out=tile_words[r][:].rearrange("p (n t) -> p n t", t=4),
                    in0=left[:, four, rows].rearrange("p t n -> p n t"),
                    in1=right[:, four, rows].rearrange("p t n -> p n t"),
                    op=ALU.max,
                )
            if r > 0:
                quantise(c, WORDS * a + 3, tile_words[r - 1], slice((r - 1) * P, r * P))
                multiply_words(c, a, 2, [r - 1])
        add_bias_and_store(c, range(R_TILES))
